import numpy as np
import ml_dtypes


def mxq(x, axis, fmt="e4m3"):
    dtype, down = {"e4m3": (ml_dtypes.float8_e4m3fn, 7), "e5m2": (ml_dtypes.float8_e5m2, 14)}[fmt]
    v = np.moveaxis(np.asarray(x, np.float32).astype(ml_dtypes.bfloat16).astype(np.float64), axis, -1)
    blocks = v.reshape(v.shape[:-1] + (-1, 32))
    amax = np.abs(blocks).max(-1, keepdims=True)
    byte = np.maximum(np.where(amax > 0, np.frexp(amax)[1] - 1 + 127, 0) - down, 1)
    scale = np.exp2(byte - 127.0)
    codes = (blocks / scale).astype(np.float32).astype(dtype).astype(np.float64)
    return np.moveaxis((codes * scale).reshape(v.shape), -1, axis)


BF16 = ml_dtypes.bfloat16


def bf(x):
    return np.asarray(x, np.float32).astype(BF16)


def f64(x):
    return np.asarray(x).astype(np.float64)


B, DIM, Z = 4, 1024, 256

TAU = 1.0


def setup_inputs():
    return {"input": bf(np.random.standard_normal((B, DIM, Z)) * 0.25 * np.sqrt(DIM)),
            "scores": bf(np.log(4.0 / DIM) + np.random.uniform(-0.75, 0.75, (B, DIM)))}


def reference(input, scores):
    e = np.exp(f64(scores))
    A = np.abs(e[:, :, None] - e[:, None, :])
    rowsum = A.sum(-1)
    scaling = DIM + 1 - 2.0 * (np.arange(DIM) + 1)
    P_max = scaling[None, :, None] * e[:, None, :] - rowsum[:, None, :]
    P_hat_raw = P_max / TAU
    ex = np.exp(P_hat_raw - P_hat_raw.max(-1, keepdims=True))
    P_hat = ex / ex.sum(-1, keepdims=True)
    out = mxq(P_hat, 2, "e4m3") @ mxq(f64(input), 1, "e4m3")
    return (out, P_hat, P_hat_raw)

@@ -1,0 +1,504 @@
+from contextlib import ExitStack
+
+import concourse.mybir as mybir
+from concourse.masks import make_identity
+
+F32 = mybir.dt.float32
+BF16 = mybir.dt.bfloat16
+U32 = mybir.dt.uint32
+U8 = mybir.dt.uint8
+FP8X4 = mybir.dt.float8_e4m3fn_x4
+ALU = mybir.AluOpType
+ACT = mybir.ActivationFunctionType
+AX = mybir.AxisListType
+
+B, DIM, Z = 4, 1024, 256
+P = 128
+NCH = DIM // P
+HALF = 512
+UNITS = B * NCH
+FLOPS = 2 * B * DIM * DIM * Z
+MANUAL = True
+E_ON_G = True
+TAIL = 24
+
+
+def NEG_ENGINE(nc):
+    return nc.gpsimd
+
+
+def tile_neuralsort_t_kernel(tc, inp, scores, out_0, out_1, out_2):
+    nc = tc.nc
+    raw_v = out_2.rearrange("b (p a) i -> b p a i", a=NCH)
+    ph_v = out_1.rearrange("b (p a) i -> b p a i", a=NCH)
+    out_v = out_0.rearrange("b (p a) z -> b p a z", a=NCH)
+    in_v = inp.rearrange("b (s p) z -> b p s z", p=P)
+
+    with ExitStack() as ctx:
+        if MANUAL:
+            ctx.enter_context(tc.manual_schedule())
+        const = ctx.enter_context(tc.tile_pool(name="const", bufs=1))
+        tpool = ctx.enter_context(tc.tile_pool(name="tpool", bufs=2))
+        rtpool = ctx.enter_context(tc.tile_pool(name="rtpool", bufs=3))
+        rowp = ctx.enter_context(tc.tile_pool(name="rowp", bufs=3))
+        exp_pool = ctx.enter_context(tc.tile_pool(name="exp_pool", bufs=2))
+        gpool = ctx.enter_context(tc.tile_pool(name="gpool", bufs=4))
+        outp = ctx.enter_context(tc.tile_pool(name="outp", bufs=2))
+        bsmall = ctx.enter_context(tc.tile_pool(name="bsmall", bufs=2))
+        usmall = ctx.enter_context(tc.tile_pool(name="usmall", bufs=4))
+        ps_raw = ctx.enter_context(tc.psum_pool(name="ps_raw", bufs=3))
+        ps_pt = ctx.enter_context(tc.psum_pool(name="ps_pt", bufs=3))
+        ps_acc = ctx.enter_context(tc.psum_pool(name="ps_acc", bufs=1))
+        ps_small = ctx.enter_context(tc.psum_pool(name="ps_small", bufs=1))
+
+        xb = const.tile([32, P], BF16, name="xb", tag="xb")
+        nc.sync.dma_start(out=xb[:], in_=scores.rearrange("b (c p) -> (b c) p", p=P))
+        scores_b = const.tile([P, B, DIM], BF16, name="scores_b", tag="scores_b")
+        in_raw = const.tile([P, B, NCH, Z], BF16, name="in_raw", tag="in_raw")
+        for b in (0, 1):
+            nc.sync.dma_start(out=scores_b[:, b, :], in_=scores[b, :].partition_broadcast(P))
+            nc.sync.dma_start(out=in_raw[:, b, :, :], in_=in_v[b])
+        for b in (2, 3):
+            nc.sync.dma_start(out=scores_b[:, b, :], in_=scores[b, :].partition_broadcast(P))
+        for b in (2, 3):
+            nc.sync.dma_start(out=in_raw[:, b, :, :], in_=in_v[b])
+
+        ident = const.tile([P, P], F32, name="ident", tag="ident")
+        make_identity(nc, ident[:])
+        s_perm = const.tile([P, DIM], F32, name="s_perm", tag="s_perm")
+        nc.gpsimd.iota(
+            s_perm[:],
+            pattern=[[-2, NCH], [-2 * NCH, P]],
+            base=DIM - 1,
+            channel_multiplier=0,
+            allow_small_or_imprecise_dtypes=True,
+        )
+        xf = const.tile([P, P], F32, name="xf", tag="xf")
+        nc.vector.memset(xf[:], 0.0)
+        ones_bf = const.tile([P, P], BF16, name="ones_bf", tag="ones_bf")
+        nc.vector.memset(ones_bf[:], 1.0)
+        parts = const.tile([P, B * NCH, 4], BF16, name="parts", tag="parts")
+        nc.vector.memset(parts[:, :, 0:1], 1.0)
+
+        nc.vector.tensor_copy(out=xf[0:32, :], in_=xb[:])
+        sc_t = ps_small.tile([P, P], F32, name="sc_t", tag="small")
+        nc.tensor.transpose(sc_t[:], xf[:], ident[:])
+        score_col = const.tile([P, B * NCH], F32, name="score_col", tag="score_col")
+        nc.vector.tensor_copy(out=score_col[:], in_=sc_t[:, 0 : B * NCH])
+        e_col = const.tile([P, B * NCH], F32, name="e_col", tag="e_col")
+        nc.scalar.activation(out=e_col[:], in_=sc_t[:, 0 : B * NCH], func=ACT.Exp)
+
+        igrp = const.tile([P, B * 2, Z, 4], BF16, name="igrp", tag="igrp", align_bytes=64)
+        icodes = const.tile([P, B * 2 * Z], U32, name="icodes", tag="icodes", align_bytes=64)
+        iscl = const.tile([P, B * 2 * Z], U8, name="iscl", tag="iscl", align_bytes=64)
+        rest1 = const.tile([P, B * NCH], F32, name="rest1", tag="rest1")
+        rest2 = const.tile([P, B * NCH], F32, name="rest2", tag="rest2")
+
+        rows = {}
+
+        def split_e(step):
+            if step == 0:
+                nc.vector.tensor_copy(out=parts[:, :, 1], in_=e_col[:])
+            elif step == 1:
+                nc.vector.tensor_tensor(out=rest1[:], in0=e_col[:], in1=parts[:, :, 1], op=ALU.subtract)
+            elif step == 2:
+                nc.vector.tensor_copy(out=parts[:, :, 2], in_=rest1[:])
+            elif step == 3:
+                nc.vector.tensor_tensor(out=rest2[:], in0=rest1[:], in1=parts[:, :, 2], op=ALU.subtract)
+            else:
+                nc.vector.tensor_copy(out=parts[:, :, 3], in_=rest2[:])
+
+        def regroup_input(b, g):
+            nc.scalar.copy(
+                out=igrp[:, 2 * b + g, :, :],
+                in_=in_raw[:, b, 4 * g : 4 * g + 4, :].rearrange("p t z -> p z t"),
+            )
+
+        def quantise_input(b):
+            nc.vector.quantize_mx(
+                out=icodes[:, 2 * Z * b : 2 * Z * (b + 1)].bitcast(FP8X4),
+                scales=iscl[:, 2 * Z * b : 2 * Z * (b + 1)],
+                in_=igrp[:, 2 * b : 2 * b + 2, :, :].rearrange("p g z t -> p (g z t)"),
+            )
+
+        def compare_v(b, ca):
+            if ca == 0:
+                rows[("cmp", b)] = tpool.tile([P, NCH, DIM], BF16, name="cmp", tag="cmp")
+            col = NCH * b + ca
+            nc.vector.tensor_scalar(
+                out=rows[("cmp", b)][:, ca, :],
+                in0=scores_b[:, b, :],
+                scalar1=score_col[:, col : col + 1],
+                scalar2=None,
+                op0=ALU.is_gt,
+            )
+
+        def compare_pe(b, ca):
+            if ca == 0:
+                rows[("ls", b)] = ps_small.tile([P, NCH + 1, NCH, 4], F32, name="ls", tag="small")
+            ls = rows[("ls", b)]
+            cmp = rows[("cmp", b)]
+            for cb in range(NCH + 1):
+                lhs = cmp[:, ca, P * cb : P * (cb + 1)] if cb < NCH else ones_bf[:]
+                nc.tensor.matmul(
+                    ls[:, cb, ca, :], lhsT=lhs, rhs=parts[:, NCH * b + ca, :], start=True, stop=True
+                )
+
+        def rowsum(b, step):
+            ls = rows[("ls", b)]
+            if step == 0:
+                cnt = bsmall.tile([P, NCH], F32, name="cnt", tag="cnt")
+                nc.vector.tensor_reduce(out=cnt[:], in_=ls[:, 0:NCH, :, 0], axis=AX.X, op=ALU.add)
+                rows[("cnt", b)] = cnt
+            elif step == 1:
+                below = bsmall.tile([P, NCH + 1], F32, name="below", tag="below")
+                nc.vector.tensor_reduce(out=below[:], in_=ls[:, :, :, 1:4], axis=AX.XY, op=ALU.add)
+                rows[("below", b)] = below
+            elif step == 2:
+                wgt = bsmall.tile([P, NCH], F32, name="wgt", tag="wgt")
+                nc.vector.tensor_scalar(
+                    out=wgt[:], in0=rows[("cnt", b)][:], scalar1=2.0, scalar2=-1.0 * DIM, op0=ALU.mult, op1=ALU.add
+                )
+                rows[("wgt", b)] = wgt
+            elif step == 3:
+                we = bsmall.tile([P, NCH], F32, name="we", tag="we")
+                nc.vector.tensor_tensor(
+                    out=we[:], in0=rows[("wgt", b)][:], in1=e_col[:, NCH * b : NCH * (b + 1)], op=ALU.mult
+                )
+                rows[("we", b)] = we
+            elif step == 4:
+                r0 = bsmall.tile([P, NCH], F32, name="r0", tag="r0")
+                nc.vector.scalar_tensor_tensor(
+                    out=r0[:], in0=rows[("below", b)][:, 0:NCH], scalar=-2.0, in1=rows[("we", b)][:],
+                    op0=ALU.mult, op1=ALU.add,
+                )
+                rows[("r0", b)] = r0
+            else:
+                rsum = bsmall.tile([P, NCH], F32, name="rsum", tag="rsum")
+                nc.vector.tensor_scalar(
+                    out=rsum[:], in0=rows[("r0", b)][:], scalar1=rows[("below", b)][:, NCH : NCH + 1],
+                    scalar2=None, op0=ALU.add,
+                )
+                rows[("rsum", b)] = rsum
+
+        def rawt(b, lo, hi, c):
+            h = lo // HALF
+            if ("rawt", b, h) not in rows:
+                rows[("rawt", b, h)] = rtpool.tile([P, NCH, HALF], F32, name="rawt", tag="rawt")
+            col = NCH * b + c
+            nc.vector.tensor_scalar(
+                out=rows[("rawt", b, h)][:, c, lo - HALF * h : hi - HALF * h],
+                in0=s_perm[:, lo:hi],
+                scalar1=e_col[:, col : col + 1],
+                scalar2=rows[("rsum", b)][:, c : c + 1],
+                op0=ALU.mult,
+                op1=ALU.subtract,
+            )
+
+        def raw_transposes(u, h):
+            b, a = divmod(u, NCH)
+            rt = rows[("rawt", b, a // 4)]
+            q = P * (a % 4)
+            rp = ps_raw.tile([P, HALF], F32, name="rp", tag="rp")
+            for c4 in range(4):
+                nc.tensor.transpose(rp[:, P * c4 : P * (c4 + 1)], rt[:, 4 * h + c4, q : q + P], ident[:])
+            rows[("rp", u, h)] = rp
+
+        def store_rows(view, tile_sb, u):
+            b, a = divmod(u, NCH)
+            if u in (0, 1, UNITS - 2, UNITS - 1):
+                nc.sync.dma_start(out=view[b, :, a, :], in_=tile_sb[:, a % 2, :])
+            elif a % 2 == 1:
+                nc.sync.dma_start(out=view[b, :, a - 1 : a + 1, :], in_=tile_sb[:])
+
+        def copy_max(u, h):
+            a = u % NCH
+            if a % 2 == 0 and h == 0:
+                rows[("raw", u // 2)] = rowp.tile([P, 2, DIM], F32, name="raw_sb", tag="raw_sb")
+            if h == 0:
+                rows[("mx", u)] = usmall.tile([P, 2], F32, name="mx", tag="mx")
+            raw_sb = rows[("raw", u // 2)]
+            nc.vector.tensor_scalar(
+                out=raw_sb[:, a % 2, HALF * h : HALF * (h + 1)],
+                in0=rows[("rp", u, h)][:],
+                scalar1=1.0,
+                scalar2=None,
+                op0=ALU.mult,
+                op1=ALU.max,
+                accum_out=rows[("mx", u)][:, h : h + 1],
+            )
+            if h == 1:
+                store_rows(raw_v, raw_sb, u)
+
+        def neg_max(u):
+            mx = rows[("mx", u)]
+            negm = usmall.tile([P, 1], F32, name="negm", tag="negm")
+            NEG_ENGINE(nc).tensor_scalar(
+                out=negm[:], in0=mx[:, 0:1], scalar1=mx[:, 1:2], scalar2=-1.0, op0=ALU.max, op1=ALU.mult
+            )
+            rows[("negm", u)] = negm
+
+        def exponent(u):
+            a = u % NCH
+            raw_sb = rows[("raw", u // 2)]
+            ex = exp_pool.tile([P, DIM], F32, name="ex", tag="ex")
+            ssum = usmall.tile([P, 1], F32, name="ssum", tag="ssum")
+            nc.scalar.activation(
+                out=ex[:], in_=raw_sb[:, a % 2, :], func=ACT.Exp, bias=rows[("negm", u)][:], scale=1.0,
+                accum_out=ssum[:],
+            )
+            rows[("ex", u)] = ex
+            rows[("ssum", u)] = ssum
+
+        def recip(u):
+            rinv = usmall.tile([P, 1], F32, name="rinv", tag="rinv")
+            nc.vector.reciprocal(rinv[:], rows[("ssum", u)][:])
+            rows[("rinv", u)] = rinv
+
+        def normalise(u, engine):
+            a = u % NCH
+            if a % 2 == 0:
+                rows[("ph", u // 2)] = rowp.tile([P, 2, DIM], F32, name="ph_sb", tag="ph_sb")
+            ph_sb = rows[("ph", u // 2)]
+            if engine == "G":
+                nc.gpsimd.tensor_scalar(
+                    out=ph_sb[:, a % 2, :], in0=rows[("ex", u)][:], scalar1=rows[("rinv", u)][:], scalar2=0.0,
+                    op0=ALU.mult, op1=ALU.add,
+                )
+            else:
+                nc.vector.tensor_scalar(
+                    out=ph_sb[:, a % 2, :], in0=rows[("ex", u)][:], scalar1=rows[("rinv", u)][:], scalar2=None,
+                    op0=ALU.mult,
+                )
+            store_rows(ph_v, ph_sb, u)
+
+        def p_transposes(u, g):
+            a = u % NCH
+            ph_sb = rows[("ph", u // 2)]
+            pt = ps_pt.tile([P, 4, P], F32, name="pt", tag="pt")
+            for t in range(4):
+                lo = HALF * g + P * t
+                nc.tensor.transpose(pt[:, t, :], ph_sb[:, a % 2, lo : lo + P], ident[:])
+            rows[("pt", u, g)] = pt
+
+        def cast(u, g, engine):
+            if ("grp", u) not in rows:
+                rows[("grp", u)] = gpool.tile([P, 2, P, 4], BF16, name="grp", tag="grp", align_bytes=64)
+            if engine == "V":
+                nc.vector.tensor_copy(
+                    out=rows[("grp", u)][:, g, :, :], in_=rows[("pt", u, g)][:].rearrange("p t j -> p j t")
+                )
+            else:
+                nc.scalar.copy(
+                    out=rows[("grp", u)][:, g, :, :], in_=rows[("pt", u, g)][:].rearrange("p t j -> p j t")
+                )
+
+        def quantise(u):
+            codes = gpool.tile([P, 2 * P], U32, name="codes", tag="codes", align_bytes=64)
+            scl = gpool.tile([P, 2 * P], U8, name="scl", tag="scl", align_bytes=64)
+            nc.vector.quantize_mx(
+                out=codes[:].bitcast(FP8X4), scales=scl[:],
+                in_=rows[("grp", u)][:].rearrange("p g j t -> p (g j t)"),
+            )
+            rows[("codes", u)] = (codes, scl)
+
+        def multiply_pair(u):
+            b = u // NCH
+            acc = ps_acc.tile([P, 2, Z], F32, name="acc", tag="acc")
+            for w in range(2):
+                codes, scl = rows[("codes", u - 1 + w)]
+                for g in range(2):
+                    lo = Z * (2 * b + g)
+                    nc.tensor.matmul_mx(
+                        out=acc[:, w, :],
+                        lhsT=codes[:, P * g : P * (g + 1)].bitcast(FP8X4),
+                        lhsT_scale=scl[:, P * g : P * (g + 1)],
+                        rhs=icodes[:, lo : lo + Z].bitcast(FP8X4),
+                        rhs_scale=iscl[:, lo : lo + Z],
+                        start=(g == 0),
+                        stop=(g == 1),
+                    )
+            rows[("acc", u)] = acc
+
+        def multiply_one(u):
+            b = u // NCH
+            acc = ps_acc.tile([P, 2, Z], F32, name="acc", tag="acc")
+            codes, scl = rows[("codes", u)]
+            for g in range(2):
+                lo = Z * (2 * b + g)
+                nc.tensor.matmul_mx(
+                    out=acc[:, 0, :],
+                    lhsT=codes[:, P * g : P * (g + 1)].bitcast(FP8X4),
+                    lhsT_scale=scl[:, P * g : P * (g + 1)],
+                    rhs=icodes[:, lo : lo + Z].bitcast(FP8X4),
+                    rhs_scale=iscl[:, lo : lo + Z],
+                    start=(g == 0),
+                    stop=(g == 1),
+                )
+            rows[("acc", u)] = acc
+
+        def out_one(u, engine):
+            b, a = divmod(u, NCH)
+            out_sb = rows[("out", b)]
+            if engine == "V":
+                nc.vector.tensor_copy(out=out_sb[:, a, :], in_=rows[("acc", u)][:, 0, :])
+            else:
+                nc.scalar.copy(out=out_sb[:, a, :], in_=rows[("acc", u)][:, 0, :])
+            nc.sync.dma_start(out=out_v[b, :, a, :], in_=out_sb[:, a, :])
+
+        def out_pair(u):
+            b, a = divmod(u, NCH)
+            if a == 1:
+                rows[("out", b)] = outp.tile([P, NCH, Z], F32, name="out_sb", tag="out_sb")
+            out_sb = rows[("out", b)]
+            nc.scalar.copy(out=out_sb[:, a - 1 : a + 1, :], in_=rows[("acc", u)][:])
+            if b == B - 1 and a >= 5:
+                nc.sync.dma_start(out=out_v[b, :, a - 1 : a + 1, :], in_=out_sb[:, a - 1 : a + 1, :])
+            elif a % 4 == 3:
+                nc.sync.dma_start(out=out_v[b, :, a - 3 : a + 1, :], in_=out_sb[:, a - 3 : a + 1, :])
+
+        for step in range(5):
+            compare_v(0, step)
+            split_e(step)
+        for ca in range(5):
+            compare_pe(0, ca)
+        for ca in range(5, NCH):
+            compare_v(0, ca)
+            compare_pe(0, ca)
+        for b in range(B):
+            for g in range(2):
+                regroup_input(b, g)
+        compare_v(1, 0)
+        compare_v(1, 1)
+        rowsum(0, 0)
+        compare_v(1, 2)
+        rowsum(0, 1)
+        rowsum(0, 2)
+        compare_v(1, 3)
+        rowsum(0, 3)
+        compare_v(1, 4)
+        rowsum(0, 4)
+        compare_v(1, 5)
+        rowsum(0, 5)
+        compare_v(1, 6)
+        for c in range(NCH):
+            rawt(0, 0, P, c)
+        raw_transposes(0, 0)
+        raw_transposes(0, 1)
+        compare_v(1, 7)
+        for c in range(NCH):
+            rawt(0, P, 2 * P, c)
+        for ca in range(NCH):
+            compare_pe(1, ca)
+
+        queue = []
+        pending = []
+        need = {}
+
+        def push_rawt(b, lo, hi):
+            for c in range(NCH):
+                queue.append(("rawt", b, lo, hi, c))
+            for a in range(lo // P, hi // P):
+                need[NCH * b + a] = len(queue)
+
+        def push_rowsum(b):
+            for step in range(6):
+                queue.append(("rowsum", b, step))
+
+        push_rawt(0, 2 * P, HALF)
+        push_rawt(0, HALF, DIM)
+        push_rowsum(1)
+        push_rawt(1, 0, HALF)
+        push_rawt(1, HALF, DIM)
+        for b in range(2, B):
+            for ca in range(NCH):
+                queue.append(("cmp", b, ca))
+            push_rowsum(b)
+            push_rawt(b, 0, HALF)
+            push_rawt(b, HALF, DIM)
+        done = [0]
+        sent = [0]
+
+        def target(k):
+            if k <= 2:
+                return 8 + 4 * k
+            return 16 + (18 * (k - 2) + 4) // 5
+
+        def fill(k, many):
+            goal = min(len(queue), max(target(k), need.get(k + 2, 0)))
+            while done[0] < goal:
+                item = queue[done[0]]
+                if item[0] == "rowsum" and item[2] == 0 and sent[0] < len(pending):
+                    break
+                done[0] += 1
+                if item[0] == "rawt":
+                    rawt(item[1], item[2], item[3], item[4])
+                elif item[0] == "cmp":
+                    compare_v(item[1], item[2])
+                    pending.append((item[1], item[2]))
+                else:
+                    rowsum(item[1], item[2])
+                if not many:
+                    break
+
+        def live(u):
+            return 0 <= u < UNITS
+
+        def e_engine(u):
+            return "G" if (E_ON_G and u < UNITS - 2) else "V"
+
+        def cast_on_v(u):
+            return u >= TAIL
+
+        for k in range(UNITS + 10):
+            if live(k - 2):
+                recip(k - 2)
+                if e_engine(k - 2) == "G":
+                    normalise(k - 2, "G")
+            if live(k):
+                copy_max(k, 0)
+                copy_max(k, 1)
+                neg_max(k)
+            if live(k - 5):
+                quantise(k - 5)
+            fill(k, False)
+            if live(k - 2) and e_engine(k - 2) == "V":
+                normalise(k - 2, "V")
+            fill(k, True)
+            if live(k - 4) and cast_on_v(k - 4):
+                cast(k - 4, 1, "V")
+            if k == 1:
+                quantise_input(0)
+            if k == 3:
+                quantise_input(1)
+            if k in (12, 20):
+                quantise_input(k // 8 + 1)
+            if k - 1 >= TAIL and live(k - 1):
+                exponent(k - 1)
+            if live(k - 4):
+                cast(k - 4, 0, "S")
+                if not cast_on_v(k - 4):
+                    cast(k - 4, 1, "S")
+            if k - 1 < TAIL and live(k - 1):
+                exponent(k - 1)
+            if live(k - 7) and (k - 7) % 2 == 1 and k - 7 != UNITS - 1:
+                out_pair(k - 7)
+            if live(k + 1):
+                raw_transposes(k + 1, 0)
+                raw_transposes(k + 1, 1)
+            if live(k - 3):
+                p_transposes(k - 3, 0)
+                p_transposes(k - 3, 1)
+            if live(k - 6) and (k - 6) % 2 == 1 and k - 6 != UNITS - 1:
+                multiply_pair(k - 6)
+            if k - 6 == UNITS - 2:
+                multiply_one(UNITS - 2)
+            if k - 6 == UNITS - 1:
+                out_one(UNITS - 2, "S")
+                multiply_one(UNITS - 1)
+            if k - 7 == UNITS - 1:
+                out_one(UNITS - 1, "V")
+            while sent[0] < len(pending):
+                compare_pe(pending[sent[0]][0], pending[sent[0]][1])
+                sent[0] += 1
+        assert done[0] == len(queue)

@@ -51,18 +51,15 @@ def tile_neuralsort_t_kernel(tc, inp, scores, out_0, out_1, out_2):
         ps_acc = ctx.enter_context(tc.psum_pool(name="ps_acc", bufs=1))
         ps_small = ctx.enter_context(tc.psum_pool(name="ps_small", bufs=1))
 
-        xb = const.tile([32, P], BF16, name="xb", tag="xb")
-        nc.sync.dma_start(out=xb[:], in_=scores.rearrange("b (c p) -> (b c) p", p=P))
-        scores_b = const.tile([P, B, DIM], BF16, name="scores_b", tag="scores_b")
+        xz = const.tile([P, P], BF16, name="xz", tag="xz")
+        nc.sync.dma_start(out=xz[0:32, :], in_=scores.rearrange("b (c p) -> (b c) p", p=P))
         in_raw = const.tile([P, B, NCH, Z], BF16, name="in_raw", tag="in_raw")
-        for b in (0, 1):
-            nc.sync.dma_start(out=scores_b[:, b, :], in_=scores[b, :].partition_broadcast(P))
-            nc.sync.dma_start(out=in_raw[:, b, :, :], in_=in_v[b])
-        for b in (2, 3):
-            nc.sync.dma_start(out=scores_b[:, b, :], in_=scores[b, :].partition_broadcast(P))
-        for b in (2, 3):
-            nc.sync.dma_start(out=in_raw[:, b, :, :], in_=in_v[b])
+        for b in range(B):
+            nc.scalar.dma_start(out=in_raw[:, b, :, :], in_=in_v[b])
+        scores_b = const.tile([P, B, DIM], BF16, name="scores_b", tag="scores_b")
 
+        ident_bf = const.tile([P, P], BF16, name="ident_bf", tag="ident_bf")
+        make_identity(nc, ident_bf[:])
         ident = const.tile([P, P], F32, name="ident", tag="ident")
         make_identity(nc, ident[:])
         s_perm = const.tile([P, DIM], F32, name="s_perm", tag="s_perm")
@@ -73,20 +70,32 @@ def tile_neuralsort_t_kernel(tc, inp, scores, out_0, out_1, out_2):
             channel_multiplier=0,
             allow_small_or_imprecise_dtypes=True,
         )
-        xf = const.tile([P, P], F32, name="xf", tag="xf")
-        nc.vector.memset(xf[:], 0.0)
+        nc.vector.memset(xz[32:64, :], 0.0)
+        nc.vector.memset(xz[64:128, :], 0.0)
         ones_bf = const.tile([P, P], BF16, name="ones_bf", tag="ones_bf")
         nc.vector.memset(ones_bf[:], 1.0)
         parts = const.tile([P, B * NCH, 4], BF16, name="parts", tag="parts")
         nc.vector.memset(parts[:, :, 0:1], 1.0)
 
-        nc.vector.tensor_copy(out=xf[0:32, :], in_=xb[:])
-        sc_t = ps_small.tile([P, P], F32, name="sc_t", tag="small")
-        nc.tensor.transpose(sc_t[:], xf[:], ident[:])
+        sc_t = ps_small.tile([P, P], BF16, name="sc_t", tag="small")
+        nc.tensor.transpose(sc_t[:], xz[:], ident_bf[:])
         score_col = const.tile([P, B * NCH], F32, name="score_col", tag="score_col")
         nc.vector.tensor_copy(out=score_col[:], in_=sc_t[:, 0 : B * NCH])
         e_col = const.tile([P, B * NCH], F32, name="e_col", tag="e_col")
         nc.scalar.activation(out=e_col[:], in_=sc_t[:, 0 : B * NCH], func=ACT.Exp)
+
+        def spread_scores(b):
+            wide = ps_pt.tile([P, DIM], BF16, name="wide", tag="pt")
+            for c in range(NCH):
+                row = NCH * b + c
+                nc.tensor.matmul(
+                    wide[:, P * c : P * (c + 1)],
+                    lhsT=ident_bf[:, row : row + 1].to_broadcast([P, P]),
+                    rhs=xz[:],
+                    start=True,
+                    stop=True,
+                )
+            nc.scalar.copy(out=scores_b[:, b, :], in_=wide[:])
 
         igrp = const.tile([P, B * 2, Z, 4], BF16, name="igrp", tag="igrp", align_bytes=64)
         icodes = const.tile([P, B * 2 * Z], U32, name="icodes", tag="icodes", align_bytes=64)
@@ -357,14 +366,20 @@ def tile_neuralsort_t_kernel(tc, inp, scores, out_0, out_1, out_2):
             elif a % 4 == 3:
                 nc.sync.dma_start(out=out_v[b, :, a - 3 : a + 1, :], in_=out_sb[:, a - 3 : a + 1, :])
 
-        for step in range(5):
+        spread_scores(0)
+        split_e(0)
+        split_e(1)
+        for step in range(3):
             compare_v(0, step)
-            split_e(step)
-        for ca in range(5):
+            split_e(step + 2)
+        spread_scores(1)
+        for ca in range(3):
             compare_pe(0, ca)
-        for ca in range(5, NCH):
+        for ca in range(3, NCH):
             compare_v(0, ca)
             compare_pe(0, ca)
+        spread_scores(2)
+        spread_scores(3)
         for b in range(B):
             for g in range(2):
                 regroup_input(b, g)

@@ -19,12 +19,12 @@ HALF = 512
 UNITS = B * NCH
 FLOPS = 2 * B * DIM * DIM * Z
 MANUAL = True
-E_ON_G = True
+G_FROM = 512
 TAIL = 24
 
 
 def NEG_ENGINE(nc):
-    return nc.gpsimd
+    return nc.vector
 
 
 def tile_neuralsort_t_kernel(tc, inp, scores, out_0, out_1, out_2):
@@ -51,15 +51,18 @@ def tile_neuralsort_t_kernel(tc, inp, scores, out_0, out_1, out_2):
         ps_acc = ctx.enter_context(tc.psum_pool(name="ps_acc", bufs=1))
         ps_small = ctx.enter_context(tc.psum_pool(name="ps_small", bufs=1))
 
-        xz = const.tile([P, P], BF16, name="xz", tag="xz")
-        nc.sync.dma_start(out=xz[0:32, :], in_=scores.rearrange("b (c p) -> (b c) p", p=P))
-        in_raw = const.tile([P, B, NCH, Z], BF16, name="in_raw", tag="in_raw")
-        for b in range(B):
-            nc.scalar.dma_start(out=in_raw[:, b, :, :], in_=in_v[b])
+        xb = const.tile([32, P], BF16, name="xb", tag="xb")
+        nc.sync.dma_start(out=xb[:], in_=scores.rearrange("b (c p) -> (b c) p", p=P))
         scores_b = const.tile([P, B, DIM], BF16, name="scores_b", tag="scores_b")
+        in_raw = const.tile([P, B, NCH, Z], BF16, name="in_raw", tag="in_raw")
+        for b in (0, 1):
+            nc.sync.dma_start(out=scores_b[:, b, :], in_=scores[b, :].partition_broadcast(P))
+            nc.sync.dma_start(out=in_raw[:, b, :, :], in_=in_v[b])
+        for b in (2, 3):
+            nc.sync.dma_start(out=scores_b[:, b, :], in_=scores[b, :].partition_broadcast(P))
+        for b in (2, 3):
+            nc.sync.dma_start(out=in_raw[:, b, :, :], in_=in_v[b])
 
-        ident_bf = const.tile([P, P], BF16, name="ident_bf", tag="ident_bf")
-        make_identity(nc, ident_bf[:])
         ident = const.tile([P, P], F32, name="ident", tag="ident")
         make_identity(nc, ident[:])
         s_perm = const.tile([P, DIM], F32, name="s_perm", tag="s_perm")
@@ -70,32 +73,20 @@ def tile_neuralsort_t_kernel(tc, inp, scores, out_0, out_1, out_2):
             channel_multiplier=0,
             allow_small_or_imprecise_dtypes=True,
         )
-        nc.vector.memset(xz[32:64, :], 0.0)
-        nc.vector.memset(xz[64:128, :], 0.0)
+        xf = const.tile([P, P], F32, name="xf", tag="xf")
+        nc.vector.memset(xf[:], 0.0)
         ones_bf = const.tile([P, P], BF16, name="ones_bf", tag="ones_bf")
         nc.vector.memset(ones_bf[:], 1.0)
         parts = const.tile([P, B * NCH, 4], BF16, name="parts", tag="parts")
         nc.vector.memset(parts[:, :, 0:1], 1.0)
 
-        sc_t = ps_small.tile([P, P], BF16, name="sc_t", tag="small")
-        nc.tensor.transpose(sc_t[:], xz[:], ident_bf[:])
+        nc.vector.tensor_copy(out=xf[0:32, :], in_=xb[:])
+        sc_t = ps_small.tile([P, P], F32, name="sc_t", tag="small")
+        nc.tensor.transpose(sc_t[:], xf[:], ident[:])
         score_col = const.tile([P, B * NCH], F32, name="score_col", tag="score_col")
         nc.vector.tensor_copy(out=score_col[:], in_=sc_t[:, 0 : B * NCH])
         e_col = const.tile([P, B * NCH], F32, name="e_col", tag="e_col")
         nc.scalar.activation(out=e_col[:], in_=sc_t[:, 0 : B * NCH], func=ACT.Exp)
-
-        def spread_scores(b):
-            wide = ps_pt.tile([P, DIM], BF16, name="wide", tag="pt")
-            for c in range(NCH):
-                row = NCH * b + c
-                nc.tensor.matmul(
-                    wide[:, P * c : P * (c + 1)],
-                    lhsT=ident_bf[:, row : row + 1].to_broadcast([P, P]),
-                    rhs=xz[:],
-                    start=True,
-                    stop=True,
-                )
-            nc.scalar.copy(out=scores_b[:, b, :], in_=wide[:])
 
         igrp = const.tile([P, B * 2, Z, 4], BF16, name="igrp", tag="igrp", align_bytes=64)
         icodes = const.tile([P, B * 2 * Z], U32, name="icodes", tag="icodes", align_bytes=64)
@@ -264,22 +255,24 @@ def tile_neuralsort_t_kernel(tc, inp, scores, out_0, out_1, out_2):
             nc.vector.reciprocal(rinv[:], rows[("ssum", u)][:])
             rows[("rinv", u)] = rinv
 
-        def normalise(u, engine):
+        def normalise(u, engine, lo, hi):
             a = u % NCH
-            if a % 2 == 0:
+            if ("ph", u // 2) not in rows:
                 rows[("ph", u // 2)] = rowp.tile([P, 2, DIM], F32, name="ph_sb", tag="ph_sb")
             ph_sb = rows[("ph", u // 2)]
             if engine == "G":
                 nc.gpsimd.tensor_scalar(
-                    out=ph_sb[:, a % 2, :], in0=rows[("ex", u)][:], scalar1=rows[("rinv", u)][:], scalar2=0.0,
-                    op0=ALU.mult, op1=ALU.add,
+                    out=ph_sb[:, a % 2, lo:hi], in0=rows[("ex", u)][:, lo:hi], scalar1=rows[("rinv", u)][:],
+                    scalar2=0.0, op0=ALU.mult, op1=ALU.add,
                 )
             else:
                 nc.vector.tensor_scalar(
-                    out=ph_sb[:, a % 2, :], in0=rows[("ex", u)][:], scalar1=rows[("rinv", u)][:], scalar2=None,
-                    op0=ALU.mult,
+                    out=ph_sb[:, a % 2, lo:hi], in0=rows[("ex", u)][:, lo:hi], scalar1=rows[("rinv", u)][:],
+                    scalar2=None, op0=ALU.mult,
                 )
-            store_rows(ph_v, ph_sb, u)
+
+        def store_p(u):
+            store_rows(ph_v, rows[("ph", u // 2)], u)
 
         def p_transposes(u, g):
             a = u % NCH
@@ -366,20 +359,14 @@ def tile_neuralsort_t_kernel(tc, inp, scores, out_0, out_1, out_2):
             elif a % 4 == 3:
                 nc.sync.dma_start(out=out_v[b, :, a - 3 : a + 1, :], in_=out_sb[:, a - 3 : a + 1, :])
 
-        spread_scores(0)
-        split_e(0)
-        split_e(1)
-        for step in range(3):
+        for step in range(5):
             compare_v(0, step)
-            split_e(step + 2)
-        spread_scores(1)
-        for ca in range(3):
+            split_e(step)
+        for ca in range(5):
             compare_pe(0, ca)
-        for ca in range(3, NCH):
+        for ca in range(5, NCH):
             compare_v(0, ca)
             compare_pe(0, ca)
-        spread_scores(2)
-        spread_scores(3)
         for b in range(B):
             for g in range(2):
                 regroup_input(b, g)
@@ -446,6 +433,8 @@ def tile_neuralsort_t_kernel(tc, inp, scores, out_0, out_1, out_2):
                 if item[0] == "rowsum" and item[2] == 0 and sent[0] < len(pending):
                     break
                 done[0] += 1
+                if item[0] == "rowsum":
+                    many = False
                 if item[0] == "rawt":
                     rawt(item[1], item[2], item[3], item[4])
                 elif item[0] == "cmp":
@@ -459,8 +448,8 @@ def tile_neuralsort_t_kernel(tc, inp, scores, out_0, out_1, out_2):
         def live(u):
             return 0 <= u < UNITS
 
-        def e_engine(u):
-            return "G" if (E_ON_G and u < UNITS - 2) else "V"
+        def g_from(u):
+            return G_FROM if u < UNITS - 2 else DIM
 
         def cast_on_v(u):
             return u >= TAIL
@@ -468,17 +457,21 @@ def tile_neuralsort_t_kernel(tc, inp, scores, out_0, out_1, out_2):
         for k in range(UNITS + 10):
             if live(k - 2):
                 recip(k - 2)
-                if e_engine(k - 2) == "G":
-                    normalise(k - 2, "G")
+                if g_from(k - 2) < DIM:
+                    normalise(k - 2, "G", g_from(k - 2), DIM)
             if live(k):
                 copy_max(k, 0)
                 copy_max(k, 1)
-                neg_max(k)
             if live(k - 5):
                 quantise(k - 5)
+            if live(k):
+                neg_max(k)
             fill(k, False)
-            if live(k - 2) and e_engine(k - 2) == "V":
-                normalise(k - 2, "V")
+            if live(k - 2):
+                if g_from(k - 2) > 0:
+                    normalise(k - 2, "V", 0, g_from(k - 2))
+                store_p(k - 2)
+            fill(k, True)
             fill(k, True)
             if live(k - 4) and cast_on_v(k - 4):
                 cast(k - 4, 1, "V")

@@ -19,12 +19,13 @@ HALF = 512
 UNITS = B * NCH
 FLOPS = 2 * B * DIM * DIM * Z
 MANUAL = True
-G_FROM = 512
+E_ON_G = True
 TAIL = 24
+DUMMIES = 2
 
 
 def NEG_ENGINE(nc):
-    return nc.vector
+    return nc.gpsimd
 
 
 def tile_neuralsort_t_kernel(tc, inp, scores, out_0, out_1, out_2):
@@ -255,24 +256,22 @@ def tile_neuralsort_t_kernel(tc, inp, scores, out_0, out_1, out_2):
             nc.vector.reciprocal(rinv[:], rows[("ssum", u)][:])
             rows[("rinv", u)] = rinv
 
-        def normalise(u, engine, lo, hi):
+        def normalise(u, engine):
             a = u % NCH
-            if ("ph", u // 2) not in rows:
+            if a % 2 == 0:
                 rows[("ph", u // 2)] = rowp.tile([P, 2, DIM], F32, name="ph_sb", tag="ph_sb")
             ph_sb = rows[("ph", u // 2)]
             if engine == "G":
                 nc.gpsimd.tensor_scalar(
-                    out=ph_sb[:, a % 2, lo:hi], in0=rows[("ex", u)][:, lo:hi], scalar1=rows[("rinv", u)][:],
-                    scalar2=0.0, op0=ALU.mult, op1=ALU.add,
+                    out=ph_sb[:, a % 2, :], in0=rows[("ex", u)][:], scalar1=rows[("rinv", u)][:], scalar2=0.0,
+                    op0=ALU.mult, op1=ALU.add,
                 )
             else:
                 nc.vector.tensor_scalar(
-                    out=ph_sb[:, a % 2, lo:hi], in0=rows[("ex", u)][:, lo:hi], scalar1=rows[("rinv", u)][:],
-                    scalar2=None, op0=ALU.mult,
+                    out=ph_sb[:, a % 2, :], in0=rows[("ex", u)][:], scalar1=rows[("rinv", u)][:], scalar2=None,
+                    op0=ALU.mult,
                 )
-
-        def store_p(u):
-            store_rows(ph_v, rows[("ph", u // 2)], u)
+            store_rows(ph_v, ph_sb, u)
 
         def p_transposes(u, g):
             a = u % NCH
@@ -323,13 +322,25 @@ def tile_neuralsort_t_kernel(tc, inp, scores, out_0, out_1, out_2):
             rows[("acc", u)] = acc
 
         def multiply_one(u):
+            acc = ps_acc.tile([P, 2 * Z], F32, name="acc", tag="acc")
+            for d in range(DUMMIES):
+                nc.tensor.matmul_mx(
+                    out=acc[:],
+                    lhsT=icodes[:, 0:P].bitcast(FP8X4),
+                    lhsT_scale=iscl[:, 0:P],
+                    rhs=icodes[:, 0 : 2 * Z].bitcast(FP8X4),
+                    rhs_scale=iscl[:, 0 : 2 * Z],
+                    start=True,
+                    stop=True,
+                )
+            if not 0 <= u < UNITS:
+                return
             b = u // NCH
-            acc = ps_acc.tile([P, 2, Z], F32, name="acc", tag="acc")
             codes, scl = rows[("codes", u)]
             for g in range(2):
                 lo = Z * (2 * b + g)
                 nc.tensor.matmul_mx(
-                    out=acc[:, 0, :],
+                    out=acc[:, 0:Z],
                     lhsT=codes[:, P * g : P * (g + 1)].bitcast(FP8X4),
                     lhsT_scale=scl[:, P * g : P * (g + 1)],
                     rhs=icodes[:, lo : lo + Z].bitcast(FP8X4),
@@ -341,12 +352,19 @@ def tile_neuralsort_t_kernel(tc, inp, scores, out_0, out_1, out_2):
 
         def out_one(u, engine):
             b, a = divmod(u, NCH)
+            if a == 0:
+                rows[("out", b)] = outp.tile([P, NCH, Z], F32, name="out_sb", tag="out_sb")
             out_sb = rows[("out", b)]
             if engine == "V":
-                nc.vector.tensor_copy(out=out_sb[:, a, :], in_=rows[("acc", u)][:, 0, :])
+                nc.vector.tensor_copy(out=out_sb[:, a, :], in_=rows[("acc", u)][:, 0:Z])
             else:
-                nc.scalar.copy(out=out_sb[:, a, :], in_=rows[("acc", u)][:, 0, :])
-            nc.sync.dma_start(out=out_v[b, :, a, :], in_=out_sb[:, a, :])
+                nc.scalar.copy(out=out_sb[:, a, :], in_=rows[("acc", u)][:, 0:Z])
+            if u >= UNITS - 2:
+                nc.sync.dma_start(out=out_v[b, :, a, :], in_=out_sb[:, a, :])
+            elif u == UNITS - 3:
+                nc.sync.dma_start(out=out_v[b, :, a - 1 : a + 1, :], in_=out_sb[:, a - 1 : a + 1, :])
+            elif a % 4 == 3:
+                nc.sync.dma_start(out=out_v[b, :, a - 3 : a + 1, :], in_=out_sb[:, a - 3 : a + 1, :])
 
         def out_pair(u):
             b, a = divmod(u, NCH)
@@ -433,8 +451,6 @@ def tile_neuralsort_t_kernel(tc, inp, scores, out_0, out_1, out_2):
                 if item[0] == "rowsum" and item[2] == 0 and sent[0] < len(pending):
                     break
                 done[0] += 1
-                if item[0] == "rowsum":
-                    many = False
                 if item[0] == "rawt":
                     rawt(item[1], item[2], item[3], item[4])
                 elif item[0] == "cmp":
@@ -448,8 +464,8 @@ def tile_neuralsort_t_kernel(tc, inp, scores, out_0, out_1, out_2):
         def live(u):
             return 0 <= u < UNITS
 
-        def g_from(u):
-            return G_FROM if u < UNITS - 2 else DIM
+        def e_engine(u):
+            return "G" if (E_ON_G and u < UNITS - 2) else "V"
 
         def cast_on_v(u):
             return u >= TAIL
@@ -457,21 +473,17 @@ def tile_neuralsort_t_kernel(tc, inp, scores, out_0, out_1, out_2):
         for k in range(UNITS + 10):
             if live(k - 2):
                 recip(k - 2)
-                if g_from(k - 2) < DIM:
-                    normalise(k - 2, "G", g_from(k - 2), DIM)
+                if e_engine(k - 2) == "G":
+                    normalise(k - 2, "G")
             if live(k):
                 copy_max(k, 0)
                 copy_max(k, 1)
+                neg_max(k)
             if live(k - 5):
                 quantise(k - 5)
-            if live(k):
-                neg_max(k)
             fill(k, False)
-            if live(k - 2):
-                if g_from(k - 2) > 0:
-                    normalise(k - 2, "V", 0, g_from(k - 2))
-                store_p(k - 2)
-            fill(k, True)
+            if live(k - 2) and e_engine(k - 2) == "V":
+                normalise(k - 2, "V")
             fill(k, True)
             if live(k - 4) and cast_on_v(k - 4):
                 cast(k - 4, 1, "V")
@@ -489,23 +501,16 @@ def tile_neuralsort_t_kernel(tc, inp, scores, out_0, out_1, out_2):
                     cast(k - 4, 1, "S")
             if k - 1 < TAIL and live(k - 1):
                 exponent(k - 1)
-            if live(k - 7) and (k - 7) % 2 == 1 and k - 7 != UNITS - 1:
-                out_pair(k - 7)
+            if live(k - 7):
+                out_one(k - 7, "V" if k - 7 == UNITS - 1 else "S")
             if live(k + 1):
                 raw_transposes(k + 1, 0)
                 raw_transposes(k + 1, 1)
+            if 2 <= k < UNITS + 6:
+                multiply_one(k - 6)
             if live(k - 3):
                 p_transposes(k - 3, 0)
                 p_transposes(k - 3, 1)
-            if live(k - 6) and (k - 6) % 2 == 1 and k - 6 != UNITS - 1:
-                multiply_pair(k - 6)
-            if k - 6 == UNITS - 2:
-                multiply_one(UNITS - 2)
-            if k - 6 == UNITS - 1:
-                out_one(UNITS - 2, "S")
-                multiply_one(UNITS - 1)
-            if k - 7 == UNITS - 1:
-                out_one(UNITS - 1, "V")
             while sent[0] < len(pending):
                 compare_pe(pending[sent[0]][0], pending[sent[0]][1])
                 sent[0] += 1

@@ -21,7 +21,6 @@ FLOPS = 2 * B * DIM * DIM * Z
 MANUAL = True
 E_ON_G = True
 TAIL = 24
-DUMMIES = 2
 
 
 def NEG_ENGINE(nc):
@@ -52,62 +51,70 @@ def tile_neuralsort_t_kernel(tc, inp, scores, out_0, out_1, out_2):
         ps_acc = ctx.enter_context(tc.psum_pool(name="ps_acc", bufs=1))
         ps_small = ctx.enter_context(tc.psum_pool(name="ps_small", bufs=1))
 
-        xb = const.tile([32, P], BF16, name="xb", tag="xb")
-        nc.sync.dma_start(out=xb[:], in_=scores.rearrange("b (c p) -> (b c) p", p=P))
-        scores_b = const.tile([P, B, DIM], BF16, name="scores_b", tag="scores_b")
+        xz = const.tile([P, P], BF16, name="xz", tag="xz")
+        nc.sync.dma_start(out=xz[0:32, :], in_=scores.rearrange("b (c p) -> (b c) p", p=P))
         in_raw = const.tile([P, B, NCH, Z], BF16, name="in_raw", tag="in_raw")
-        for b in (0, 1):
-            nc.sync.dma_start(out=scores_b[:, b, :], in_=scores[b, :].partition_broadcast(P))
-            nc.sync.dma_start(out=in_raw[:, b, :, :], in_=in_v[b])
-        for b in (2, 3):
-            nc.sync.dma_start(out=scores_b[:, b, :], in_=scores[b, :].partition_broadcast(P))
-        for b in (2, 3):
-            nc.sync.dma_start(out=in_raw[:, b, :, :], in_=in_v[b])
+        for b in range(B):
+            nc.scalar.dma_start(out=in_raw[:, b, :, :], in_=in_v[b])
+        scores_b = const.tile([P, B, DIM], BF16, name="scores_b", tag="scores_b")
 
+        ident_bf = const.tile([P, P], BF16, name="ident_bf", tag="ident_bf")
+        make_identity(nc, ident_bf[:])
         ident = const.tile([P, P], F32, name="ident", tag="ident")
         make_identity(nc, ident[:])
         s_perm = const.tile([P, DIM], F32, name="s_perm", tag="s_perm")
         nc.gpsimd.iota(
             s_perm[:],
             pattern=[[-2, NCH], [-2 * NCH, P]],
-            base=DIM - 1,
+            base=2 * DIM - 1,
             channel_multiplier=0,
             allow_small_or_imprecise_dtypes=True,
         )
-        xf = const.tile([P, P], F32, name="xf", tag="xf")
-        nc.vector.memset(xf[:], 0.0)
+        nc.vector.memset(xz[32:64, :], 0.0)
+        nc.vector.memset(xz[64:128, :], 0.0)
         ones_bf = const.tile([P, P], BF16, name="ones_bf", tag="ones_bf")
         nc.vector.memset(ones_bf[:], 1.0)
         parts = const.tile([P, B * NCH, 4], BF16, name="parts", tag="parts")
         nc.vector.memset(parts[:, :, 0:1], 1.0)
 
-        nc.vector.tensor_copy(out=xf[0:32, :], in_=xb[:])
-        sc_t = ps_small.tile([P, P], F32, name="sc_t", tag="small")
-        nc.tensor.transpose(sc_t[:], xf[:], ident[:])
+        sc_t = ps_small.tile([P, P], BF16, name="sc_t", tag="small")
+        nc.tensor.transpose(sc_t[:], xz[:], ident_bf[:])
         score_col = const.tile([P, B * NCH], F32, name="score_col", tag="score_col")
         nc.vector.tensor_copy(out=score_col[:], in_=sc_t[:, 0 : B * NCH])
         e_col = const.tile([P, B * NCH], F32, name="e_col", tag="e_col")
         nc.scalar.activation(out=e_col[:], in_=sc_t[:, 0 : B * NCH], func=ACT.Exp)
+        e_hi = const.tile([P, B * NCH], BF16, name="e_hi", tag="e_hi")
+        nc.scalar.activation(out=e_hi[:], in_=sc_t[:, 0 : B * NCH], func=ACT.Exp)
+
+        def spread_scores(b):
+            wide = ps_pt.tile([P, DIM], BF16, name="wide", tag="pt")
+            for c in range(NCH):
+                row = NCH * b + c
+                nc.tensor.matmul(
+                    wide[:, P * c : P * (c + 1)],
+                    lhsT=ident_bf[:, row : row + 1].to_broadcast([P, P]),
+                    rhs=xz[:],
+                    start=True,
+                    stop=True,
+                )
+            nc.scalar.copy(out=scores_b[:, b, :], in_=wide[:])
 
         igrp = const.tile([P, B * 2, Z, 4], BF16, name="igrp", tag="igrp", align_bytes=64)
         icodes = const.tile([P, B * 2 * Z], U32, name="icodes", tag="icodes", align_bytes=64)
         iscl = const.tile([P, B * 2 * Z], U8, name="iscl", tag="iscl", align_bytes=64)
         rest1 = const.tile([P, B * NCH], F32, name="rest1", tag="rest1")
-        rest2 = const.tile([P, B * NCH], F32, name="rest2", tag="rest2")
 
         rows = {}
 
         def split_e(step):
             if step == 0:
-                nc.vector.tensor_copy(out=parts[:, :, 1], in_=e_col[:])
+                nc.vector.tensor_tensor(out=rest1[:], in0=e_col[:], in1=e_hi[:], op=ALU.subtract)
             elif step == 1:
-                nc.vector.tensor_tensor(out=rest1[:], in0=e_col[:], in1=parts[:, :, 1], op=ALU.subtract)
+                nc.vector.tensor_tensor(out=parts[:, :, 2], in0=e_col[:], in1=e_hi[:], op=ALU.subtract)
             elif step == 2:
-                nc.vector.tensor_copy(out=parts[:, :, 2], in_=rest1[:])
-            elif step == 3:
-                nc.vector.tensor_tensor(out=rest2[:], in0=rest1[:], in1=parts[:, :, 2], op=ALU.subtract)
+                nc.vector.tensor_copy(out=parts[:, :, 1], in_=e_hi[:])
             else:
-                nc.vector.tensor_copy(out=parts[:, :, 3], in_=rest2[:])
+                nc.vector.tensor_tensor(out=parts[:, :, 3], in0=rest1[:], in1=parts[:, :, 2], op=ALU.subtract)
 
         def regroup_input(b, g):
             nc.scalar.copy(
@@ -156,30 +163,22 @@ def tile_neuralsort_t_kernel(tc, inp, scores, out_0, out_1, out_2):
                 nc.vector.tensor_reduce(out=below[:], in_=ls[:, :, :, 1:4], axis=AX.XY, op=ALU.add)
                 rows[("below", b)] = below
             elif step == 2:
-                wgt = bsmall.tile([P, NCH], F32, name="wgt", tag="wgt")
-                nc.vector.tensor_scalar(
-                    out=wgt[:], in0=rows[("cnt", b)][:], scalar1=2.0, scalar2=-1.0 * DIM, op0=ALU.mult, op1=ALU.add
-                )
-                rows[("wgt", b)] = wgt
-            elif step == 3:
-                we = bsmall.tile([P, NCH], F32, name="we", tag="we")
-                nc.vector.tensor_tensor(
-                    out=we[:], in0=rows[("wgt", b)][:], in1=e_col[:, NCH * b : NCH * (b + 1)], op=ALU.mult
-                )
-                rows[("we", b)] = we
-            elif step == 4:
-                r0 = bsmall.tile([P, NCH], F32, name="r0", tag="r0")
+                x1 = bsmall.tile([P, NCH], F32, name="x1", tag="x1")
                 nc.vector.scalar_tensor_tensor(
-                    out=r0[:], in0=rows[("below", b)][:, 0:NCH], scalar=-2.0, in1=rows[("we", b)][:],
-                    op0=ALU.mult, op1=ALU.add,
+                    out=x1[:], in0=rows[("cnt", b)][:], scalar=2.0, in1=e_col[:, NCH * b : NCH * (b + 1)],
+                    op0=ALU.mult, op1=ALU.mult,
                 )
-                rows[("r0", b)] = r0
+                rows[("x1", b)] = x1
+            elif step == 3:
+                x2 = bsmall.tile([P, NCH], F32, name="x2", tag="x2")
+                nc.vector.tensor_scalar(
+                    out=x2[:], in0=rows[("below", b)][:, 0:NCH], scalar1=-2.0,
+                    scalar2=rows[("below", b)][:, NCH : NCH + 1], op0=ALU.mult, op1=ALU.add,
+                )
+                rows[("x2", b)] = x2
             else:
                 rsum = bsmall.tile([P, NCH], F32, name="rsum", tag="rsum")
-                nc.vector.tensor_scalar(
-                    out=rsum[:], in0=rows[("r0", b)][:], scalar1=rows[("below", b)][:, NCH : NCH + 1],
-                    scalar2=None, op0=ALU.add,
-                )
+                nc.vector.tensor_tensor(out=rsum[:], in0=rows[("x1", b)][:], in1=rows[("x2", b)][:], op=ALU.add)
                 rows[("rsum", b)] = rsum
 
         def rawt(b, lo, hi, c):
@@ -322,25 +321,13 @@ def tile_neuralsort_t_kernel(tc, inp, scores, out_0, out_1, out_2):
             rows[("acc", u)] = acc
 
         def multiply_one(u):
-            acc = ps_acc.tile([P, 2 * Z], F32, name="acc", tag="acc")
-            for d in range(DUMMIES):
-                nc.tensor.matmul_mx(
-                    out=acc[:],
-                    lhsT=icodes[:, 0:P].bitcast(FP8X4),
-                    lhsT_scale=iscl[:, 0:P],
-                    rhs=icodes[:, 0 : 2 * Z].bitcast(FP8X4),
-                    rhs_scale=iscl[:, 0 : 2 * Z],
-                    start=True,
-                    stop=True,
-                )
-            if not 0 <= u < UNITS:
-                return
             b = u // NCH
+            acc = ps_acc.tile([P, 2, Z], F32, name="acc", tag="acc")
             codes, scl = rows[("codes", u)]
             for g in range(2):
                 lo = Z * (2 * b + g)
                 nc.tensor.matmul_mx(
-                    out=acc[:, 0:Z],
+                    out=acc[:, 0, :],
                     lhsT=codes[:, P * g : P * (g + 1)].bitcast(FP8X4),
                     lhsT_scale=scl[:, P * g : P * (g + 1)],
                     rhs=icodes[:, lo : lo + Z].bitcast(FP8X4),
@@ -352,19 +339,12 @@ def tile_neuralsort_t_kernel(tc, inp, scores, out_0, out_1, out_2):
 
         def out_one(u, engine):
             b, a = divmod(u, NCH)
-            if a == 0:
-                rows[("out", b)] = outp.tile([P, NCH, Z], F32, name="out_sb", tag="out_sb")
             out_sb = rows[("out", b)]
             if engine == "V":
-                nc.vector.tensor_copy(out=out_sb[:, a, :], in_=rows[("acc", u)][:, 0:Z])
+                nc.vector.tensor_copy(out=out_sb[:, a, :], in_=rows[("acc", u)][:, 0, :])
             else:
-                nc.scalar.copy(out=out_sb[:, a, :], in_=rows[("acc", u)][:, 0:Z])
-            if u >= UNITS - 2:
-                nc.sync.dma_start(out=out_v[b, :, a, :], in_=out_sb[:, a, :])
-            elif u == UNITS - 3:
-                nc.sync.dma_start(out=out_v[b, :, a - 1 : a + 1, :], in_=out_sb[:, a - 1 : a + 1, :])
-            elif a % 4 == 3:
-                nc.sync.dma_start(out=out_v[b, :, a - 3 : a + 1, :], in_=out_sb[:, a - 3 : a + 1, :])
+                nc.scalar.copy(out=out_sb[:, a, :], in_=rows[("acc", u)][:, 0, :])
+            nc.sync.dma_start(out=out_v[b, :, a, :], in_=out_sb[:, a, :])
 
         def out_pair(u):
             b, a = divmod(u, NCH)
@@ -377,12 +357,18 @@ def tile_neuralsort_t_kernel(tc, inp, scores, out_0, out_1, out_2):
             elif a % 4 == 3:
                 nc.sync.dma_start(out=out_v[b, :, a - 3 : a + 1, :], in_=out_sb[:, a - 3 : a + 1, :])
 
-        for step in range(5):
-            compare_v(0, step)
-            split_e(step)
-        for ca in range(5):
+        for b in range(B):
+            spread_scores(b)
+        split_e(0)
+        split_e(1)
+        compare_v(0, 0)
+        split_e(2)
+        compare_v(0, 1)
+        split_e(3)
+        compare_v(0, 2)
+        for ca in range(3):
             compare_pe(0, ca)
-        for ca in range(5, NCH):
+        for ca in range(3, NCH):
             compare_v(0, ca)
             compare_pe(0, ca)
         for b in range(B):
@@ -391,23 +377,24 @@ def tile_neuralsort_t_kernel(tc, inp, scores, out_0, out_1, out_2):
         compare_v(1, 0)
         compare_v(1, 1)
         rowsum(0, 0)
-        compare_v(1, 2)
         rowsum(0, 1)
-        rowsum(0, 2)
+        compare_v(1, 2)
         compare_v(1, 3)
+        rowsum(0, 2)
         rowsum(0, 3)
         compare_v(1, 4)
-        rowsum(0, 4)
         compare_v(1, 5)
-        rowsum(0, 5)
+        rowsum(0, 4)
         compare_v(1, 6)
+        compare_v(1, 7)
         for c in range(NCH):
             rawt(0, 0, P, c)
         raw_transposes(0, 0)
         raw_transposes(0, 1)
-        compare_v(1, 7)
         for c in range(NCH):
             rawt(0, P, 2 * P, c)
+        raw_transposes(1, 0)
+        raw_transposes(1, 1)
         for ca in range(NCH):
             compare_pe(1, ca)
 
@@ -415,34 +402,41 @@ def tile_neuralsort_t_kernel(tc, inp, scores, out_0, out_1, out_2):
         pending = []
         need = {}
 
-        def push_rawt(b, lo, hi):
-            for c in range(NCH):
-                queue.append(("rawt", b, lo, hi, c))
+        def mark(b, lo, hi):
             for a in range(lo // P, hi // P):
                 need[NCH * b + a] = len(queue)
 
-        def push_rowsum(b):
-            for step in range(6):
-                queue.append(("rowsum", b, step))
+        def push_rawt(b, lo, hi):
+            for c in range(NCH):
+                queue.append(("rawt", b, lo, hi, c))
+            mark(b, lo, hi)
+
+        def push_woven(b):
+            for c in range(NCH):
+                if c in (2, 4):
+                    queue.append(("rowsum", b, c - 2))
+                    queue.append(("rowsum", b, c - 1))
+                if c == 6:
+                    queue.append(("rowsum", b, 4))
+                queue.append(("rawt", b - 1, HALF, DIM, c))
+            mark(b - 1, HALF, DIM)
 
         push_rawt(0, 2 * P, HALF)
-        push_rawt(0, HALF, DIM)
-        push_rowsum(1)
+        push_woven(1)
         push_rawt(1, 0, HALF)
-        push_rawt(1, HALF, DIM)
         for b in range(2, B):
             for ca in range(NCH):
                 queue.append(("cmp", b, ca))
-            push_rowsum(b)
+            push_woven(b)
             push_rawt(b, 0, HALF)
-            push_rawt(b, HALF, DIM)
+        push_rawt(B - 1, HALF, DIM)
         done = [0]
         sent = [0]
 
         def target(k):
             if k <= 2:
-                return 8 + 4 * k
-            return 16 + (18 * (k - 2) + 4) // 5
+                return 8 + 7 * k
+            return 22 + (18 * (k - 2) + 4) // 5
 
         def fill(k, many):
             goal = min(len(queue), max(target(k), need.get(k + 2, 0)))
@@ -501,16 +495,23 @@ def tile_neuralsort_t_kernel(tc, inp, scores, out_0, out_1, out_2):
                     cast(k - 4, 1, "S")
             if k - 1 < TAIL and live(k - 1):
                 exponent(k - 1)
-            if live(k - 7):
-                out_one(k - 7, "V" if k - 7 == UNITS - 1 else "S")
-            if live(k + 1):
+            if live(k - 7) and (k - 7) % 2 == 1 and k - 7 != UNITS - 1:
+                out_pair(k - 7)
+            if live(k + 1) and k + 1 != 1:
                 raw_transposes(k + 1, 0)
                 raw_transposes(k + 1, 1)
-            if 2 <= k < UNITS + 6:
-                multiply_one(k - 6)
             if live(k - 3):
                 p_transposes(k - 3, 0)
                 p_transposes(k - 3, 1)
+            if live(k - 6) and (k - 6) % 2 == 1 and k - 6 != UNITS - 1:
+                multiply_pair(k - 6)
+            if k - 6 == UNITS - 2:
+                multiply_one(UNITS - 2)
+            if k - 6 == UNITS - 1:
+                out_one(UNITS - 2, "S")
+                multiply_one(UNITS - 1)
+            if k - 7 == UNITS - 1:
+                out_one(UNITS - 1, "V")
             while sent[0] < len(pending):
                 compare_pe(pending[sent[0]][0], pending[sent[0]][1])
                 sent[0] += 1

@@ -5,6 +5,7 @@ from concourse.masks import make_identity
 
 F32 = mybir.dt.float32
 BF16 = mybir.dt.bfloat16
+I32 = mybir.dt.int32
 U32 = mybir.dt.uint32
 U8 = mybir.dt.uint8
 FP8X4 = mybir.dt.float8_e4m3fn_x4
@@ -18,13 +19,8 @@ NCH = DIM // P
 HALF = 512
 UNITS = B * NCH
 FLOPS = 2 * B * DIM * DIM * Z
-MANUAL = True
-E_ON_G = True
-TAIL = 24
-
-
-def NEG_ENGINE(nc):
-    return nc.gpsimd
+AHEAD = 2
+V_CASTS_FROM = 22
 
 
 def tile_neuralsort_t_kernel(tc, inp, scores, out_0, out_1, out_2):
@@ -35,43 +31,53 @@ def tile_neuralsort_t_kernel(tc, inp, scores, out_0, out_1, out_2):
     in_v = inp.rearrange("b (s p) z -> b p s z", p=P)
 
     with ExitStack() as ctx:
-        if MANUAL:
-            ctx.enter_context(tc.manual_schedule())
+        ctx.enter_context(tc.manual_schedule())
         const = ctx.enter_context(tc.tile_pool(name="const", bufs=1))
         tpool = ctx.enter_context(tc.tile_pool(name="tpool", bufs=2))
-        rtpool = ctx.enter_context(tc.tile_pool(name="rtpool", bufs=3))
-        rowp = ctx.enter_context(tc.tile_pool(name="rowp", bufs=3))
-        exp_pool = ctx.enter_context(tc.tile_pool(name="exp_pool", bufs=2))
+        rawp = ctx.enter_context(tc.tile_pool(name="rawp", bufs=5))
+        php = ctx.enter_context(tc.tile_pool(name="php", bufs=3))
+        exp_pool = ctx.enter_context(tc.tile_pool(name="exp_pool", bufs=3))
         gpool = ctx.enter_context(tc.tile_pool(name="gpool", bufs=4))
         outp = ctx.enter_context(tc.tile_pool(name="outp", bufs=2))
         bsmall = ctx.enter_context(tc.tile_pool(name="bsmall", bufs=2))
         usmall = ctx.enter_context(tc.tile_pool(name="usmall", bufs=4))
-        ps_raw = ctx.enter_context(tc.psum_pool(name="ps_raw", bufs=3))
-        ps_pt = ctx.enter_context(tc.psum_pool(name="ps_pt", bufs=3))
+        ps_rb = ctx.enter_context(tc.psum_pool(name="ps_rb", bufs=1))
+        ps_pt = ctx.enter_context(tc.psum_pool(name="ps_pt", bufs=4))
         ps_acc = ctx.enter_context(tc.psum_pool(name="ps_acc", bufs=1))
         ps_small = ctx.enter_context(tc.psum_pool(name="ps_small", bufs=1))
 
         xz = const.tile([P, P], BF16, name="xz", tag="xz")
         nc.sync.dma_start(out=xz[0:32, :], in_=scores.rearrange("b (c p) -> (b c) p", p=P))
-        in_raw = const.tile([P, B, NCH, Z], BF16, name="in_raw", tag="in_raw")
+        scores_b = []
         for b in range(B):
-            nc.scalar.dma_start(out=in_raw[:, b, :, :], in_=in_v[b])
-        scores_b = const.tile([P, B, DIM], BF16, name="scores_b", tag="scores_b")
+            sb = const.tile([P, DIM], BF16, name="scores_b%d" % b, tag="scores_b%d" % b)
+            nc.sync.dma_start(out=sb[:], in_=scores[b].partition_broadcast(P))
+            scores_b.append(sb)
+        in_raw = []
+        for b in range(B):
+            ir = const.tile([P, NCH, Z], BF16, name="in_raw%d" % b, tag="in_raw%d" % b)
+            nc.sync.dma_start(out=ir[:], in_=in_v[b])
+            in_raw.append(ir)
 
+        nc.vector.memset(xz[32:64, :], 0.0)
+        nc.vector.memset(xz[64:128, :], 0.0)
         ident_bf = const.tile([P, P], BF16, name="ident_bf", tag="ident_bf")
         make_identity(nc, ident_bf[:])
         ident = const.tile([P, P], F32, name="ident", tag="ident")
         make_identity(nc, ident[:])
-        s_perm = const.tile([P, DIM], F32, name="s_perm", tag="s_perm")
+        s_col = const.tile([P, NCH], F32, name="s_col", tag="s_col")
         nc.gpsimd.iota(
-            s_perm[:],
-            pattern=[[-2, NCH], [-2 * NCH, P]],
-            base=2 * DIM - 1,
-            channel_multiplier=0,
+            s_col[:], pattern=[[-2, NCH]], base=2 * DIM - 1, channel_multiplier=-2 * NCH,
             allow_small_or_imprecise_dtypes=True,
         )
-        nc.vector.memset(xz[32:64, :], 0.0)
-        nc.vector.memset(xz[64:128, :], 0.0)
+        rev_hi = const.tile([P, P], BF16, name="rev_hi", tag="rev_hi")
+        nc.gpsimd.iota(
+            rev_hi[:], pattern=[[-1, P]], base=P - 1, channel_multiplier=0, allow_small_or_imprecise_dtypes=True
+        )
+        rev_lo = const.tile([P, NCH], F32, name="rev_lo", tag="rev_lo")
+        nc.gpsimd.iota(
+            rev_lo[:], pattern=[[-1, NCH]], base=NCH - 1, channel_multiplier=0, allow_small_or_imprecise_dtypes=True
+        )
         ones_bf = const.tile([P, P], BF16, name="ones_bf", tag="ones_bf")
         nc.vector.memset(ones_bf[:], 1.0)
         parts = const.tile([P, B * NCH, 4], BF16, name="parts", tag="parts")
@@ -86,23 +92,12 @@ def tile_neuralsort_t_kernel(tc, inp, scores, out_0, out_1, out_2):
         e_hi = const.tile([P, B * NCH], BF16, name="e_hi", tag="e_hi")
         nc.scalar.activation(out=e_hi[:], in_=sc_t[:, 0 : B * NCH], func=ACT.Exp)
 
-        def spread_scores(b):
-            wide = ps_pt.tile([P, DIM], BF16, name="wide", tag="pt")
-            for c in range(NCH):
-                row = NCH * b + c
-                nc.tensor.matmul(
-                    wide[:, P * c : P * (c + 1)],
-                    lhsT=ident_bf[:, row : row + 1].to_broadcast([P, P]),
-                    rhs=xz[:],
-                    start=True,
-                    stop=True,
-                )
-            nc.scalar.copy(out=scores_b[:, b, :], in_=wide[:])
-
         igrp = const.tile([P, B * 2, Z, 4], BF16, name="igrp", tag="igrp", align_bytes=64)
         icodes = const.tile([P, B * 2 * Z], U32, name="icodes", tag="icodes", align_bytes=64)
         iscl = const.tile([P, B * 2 * Z], U8, name="iscl", tag="iscl", align_bytes=64)
         rest1 = const.tile([P, B * NCH], F32, name="rest1", tag="rest1")
+        t_all = const.tile([P, B], F32, name="t_all", tag="t_all")
+        e_b = [const.tile([P, DIM], F32, name="e_b%d" % b, tag="e_b%d" % b) for b in range(B)]
 
         rows = {}
 
@@ -116,11 +111,32 @@ def tile_neuralsort_t_kernel(tc, inp, scores, out_0, out_1, out_2):
             else:
                 nc.vector.tensor_tensor(out=parts[:, :, 3], in0=rest1[:], in1=parts[:, :, 2], op=ALU.subtract)
 
-        def regroup_input(b, g):
-            nc.scalar.copy(
-                out=igrp[:, 2 * b + g, :, :],
-                in_=in_raw[:, b, 4 * g : 4 * g + 4, :].rearrange("p t z -> p z t"),
+        def total_pe():
+            tot = ps_small.tile([P, B * NCH * 4], F32, name="tot", tag="small")
+            nc.tensor.matmul(
+                tot[:], lhsT=ones_bf[:], rhs=parts[:].rearrange("p c t -> p (c t)"), start=True, stop=True
             )
+            rows["tot"] = tot
+
+        def total_v():
+            nc.vector.tensor_reduce(
+                out=t_all[:],
+                in_=rows["tot"][:].rearrange("p (b c t) -> p b c t", b=B, t=4)[:, :, :, 1:4],
+                axis=AX.XY,
+                op=ALU.add,
+            )
+
+        def spread_e(b):
+            nc.scalar.activation(out=e_b[b][:], in_=scores_b[b][:], func=ACT.Exp)
+
+        def regroup_input(b, g, engine):
+            src = in_raw[b][:, 4 * g : 4 * g + 4, :].rearrange("p t z -> p z t")
+            if engine == "S":
+                nc.scalar.copy(out=igrp[:, 2 * b + g, :, :], in_=src)
+            else:
+                nc.gpsimd.tensor_scalar(
+                    out=igrp[:, 2 * b + g, :, :], in0=src, scalar1=1.0, scalar2=0.0, op0=ALU.mult, op1=ALU.add
+                )
 
         def quantise_input(b):
             nc.vector.quantize_mx(
@@ -129,80 +145,171 @@ def tile_neuralsort_t_kernel(tc, inp, scores, out_0, out_1, out_2):
                 in_=igrp[:, 2 * b : 2 * b + 2, :, :].rearrange("p g z t -> p (g z t)"),
             )
 
+        def tie_v(b):
+            eq = tpool.tile([P, NCH, P], BF16, name="eq", tag="eq")
+            for c in range(NCH):
+                nc.vector.tensor_scalar(
+                    out=eq[:, c, :], in0=scores_b[b][:, P * c : P * (c + 1)],
+                    scalar1=score_col[:, NCH * b + c : NCH * b + c + 1], scalar2=None, op0=ALU.is_equal,
+                )
+            nc.gpsimd.affine_select(
+                out=eq[:], in_=eq[:], pattern=[[0, NCH], [-1, P]], compare_op=ALU.is_gt, fill=0.0,
+                base=0, channel_multiplier=1,
+            )
+            rows[("eq", b)] = eq
+
         def compare_v(b, ca):
             if ca == 0:
                 rows[("cmp", b)] = tpool.tile([P, NCH, DIM], BF16, name="cmp", tag="cmp")
+            cmp = rows[("cmp", b)]
             col = NCH * b + ca
+            if ca:
+                nc.vector.tensor_scalar(
+                    out=cmp[:, ca, 0 : P * ca], in0=scores_b[b][:, 0 : P * ca],
+                    scalar1=score_col[:, col : col + 1], scalar2=None, op0=ALU.is_ge,
+                )
             nc.vector.tensor_scalar(
-                out=rows[("cmp", b)][:, ca, :],
-                in0=scores_b[:, b, :],
-                scalar1=score_col[:, col : col + 1],
-                scalar2=None,
-                op0=ALU.is_gt,
+                out=cmp[:, ca, P * ca : DIM], in0=scores_b[b][:, P * ca : DIM],
+                scalar1=score_col[:, col : col + 1], scalar2=None, op0=ALU.is_gt,
             )
 
         def compare_pe(b, ca):
             if ca == 0:
-                rows[("ls", b)] = ps_small.tile([P, NCH + 1, NCH, 4], F32, name="ls", tag="small")
+                rows[("ls", b)] = ps_small.tile([P, NCH, NCH + 1, 4], F32, name="ls", tag="small")
             ls = rows[("ls", b)]
             cmp = rows[("cmp", b)]
-            for cb in range(NCH + 1):
-                lhs = cmp[:, ca, P * cb : P * (cb + 1)] if cb < NCH else ones_bf[:]
+            for cb in range(NCH):
                 nc.tensor.matmul(
-                    ls[:, cb, ca, :], lhsT=lhs, rhs=parts[:, NCH * b + ca, :], start=True, stop=True
+                    ls[:, cb, ca, :], lhsT=cmp[:, ca, P * cb : P * (cb + 1)], rhs=parts[:, NCH * b + ca, :],
+                    start=True, stop=True,
                 )
+
+        def tie_pe(b):
+            ls = rows[("ls", b)]
+            for c in range(NCH):
+                nc.tensor.matmul(
+                    ls[:, c, NCH, :], lhsT=rows[("eq", b)][:, c, :], rhs=parts[:, NCH * b + c, :],
+                    start=True, stop=True,
+                )
+
+        def small(key, b, shape, dtype=F32):
+            t = bsmall.tile(shape, dtype, name=key, tag=key)
+            rows[(key, b)] = t
+            return t
 
         def rowsum(b, step):
             ls = rows[("ls", b)]
+            e = e_col[:, NCH * b : NCH * (b + 1)]
             if step == 0:
-                cnt = bsmall.tile([P, NCH], F32, name="cnt", tag="cnt")
-                nc.vector.tensor_reduce(out=cnt[:], in_=ls[:, 0:NCH, :, 0], axis=AX.X, op=ALU.add)
-                rows[("cnt", b)] = cnt
+                nc.vector.tensor_reduce(
+                    out=small("cnt", b, [P, NCH])[:], in_=ls[:, :, :, 0], axis=AX.X, op=ALU.add
+                )
             elif step == 1:
-                below = bsmall.tile([P, NCH + 1], F32, name="below", tag="below")
-                nc.vector.tensor_reduce(out=below[:], in_=ls[:, :, :, 1:4], axis=AX.XY, op=ALU.add)
-                rows[("below", b)] = below
+                nc.vector.tensor_reduce(
+                    out=small("below", b, [P, NCH])[:], in_=ls[:, :, :, 1:4], axis=AX.XY, op=ALU.add
+                )
             elif step == 2:
-                x1 = bsmall.tile([P, NCH], F32, name="x1", tag="x1")
                 nc.vector.scalar_tensor_tensor(
-                    out=x1[:], in0=rows[("cnt", b)][:], scalar=2.0, in1=e_col[:, NCH * b : NCH * (b + 1)],
+                    out=small("x1", b, [P, NCH])[:], in0=rows[("cnt", b)][:], scalar=2.0, in1=e,
                     op0=ALU.mult, op1=ALU.mult,
                 )
-                rows[("x1", b)] = x1
             elif step == 3:
-                x2 = bsmall.tile([P, NCH], F32, name="x2", tag="x2")
                 nc.vector.tensor_scalar(
-                    out=x2[:], in0=rows[("below", b)][:, 0:NCH], scalar1=-2.0,
-                    scalar2=rows[("below", b)][:, NCH : NCH + 1], op0=ALU.mult, op1=ALU.add,
+                    out=small("x2", b, [P, NCH])[:], in0=rows[("below", b)][:], scalar1=-2.0,
+                    scalar2=t_all[:, b : b + 1], op0=ALU.mult, op1=ALU.add,
                 )
-                rows[("x2", b)] = x2
             else:
-                rsum = bsmall.tile([P, NCH], F32, name="rsum", tag="rsum")
-                nc.vector.tensor_tensor(out=rsum[:], in0=rows[("x1", b)][:], in1=rows[("x2", b)][:], op=ALU.add)
-                rows[("rsum", b)] = rsum
+                nc.vector.tensor_tensor(
+                    out=small("rsum", b, [P, NCH])[:], in0=rows[("x1", b)][:], in1=rows[("x2", b)][:], op=ALU.add
+                )
 
-        def rawt(b, lo, hi, c):
-            h = lo // HALF
-            if ("rawt", b, h) not in rows:
-                rows[("rawt", b, h)] = rtpool.tile([P, NCH, HALF], F32, name="rawt", tag="rawt")
-            col = NCH * b + c
-            nc.vector.tensor_scalar(
-                out=rows[("rawt", b, h)][:, c, lo - HALF * h : hi - HALF * h],
-                in0=s_perm[:, lo:hi],
-                scalar1=e_col[:, col : col + 1],
-                scalar2=rows[("rsum", b)][:, c : c + 1],
-                op0=ALU.mult,
-                op1=ALU.subtract,
+        def spread_rowsum(b):
+            for h in range(2):
+                rb = ps_rb.tile([P, HALF], F32, name="rb%d" % h, tag="rb%d" % h)
+                for c in range(4):
+                    col = 4 * h + c
+                    nc.tensor.transpose(
+                        rb[:, P * c : P * (c + 1)],
+                        rows[("rsum", b)][:, col : col + 1].to_broadcast([P, P]),
+                        ident[:],
+                    )
+                rows[("rb", b, h)] = rb
+
+        def rank(b, step):
+            if step == 0:
+                nc.vector.tensor_copy(out=small("cnt_i", b, [P, NCH], I32)[:], in_=rows[("cnt", b)][:])
+            elif step == 1:
+                nc.vector.tensor_tensor(
+                    out=small("nm", b, [P, NCH])[:], in0=rows[("x2", b)][:], in1=e_col[:, NCH * b : NCH * (b + 1)],
+                    op=ALU.subtract,
+                )
+            elif step == 2:
+                nc.vector.tensor_scalar(
+                    out=small("hl_i", b, [P, 2, NCH], I32)[:, 0, :], in0=rows[("cnt_i", b)][:], scalar1=3,
+                    scalar2=None, op0=ALU.arith_shift_right,
+                )
+            elif step == 3:
+                nc.vector.tensor_scalar(
+                    out=rows[("hl_i", b)][:, 1, :], in0=rows[("cnt_i", b)][:], scalar1=7,
+                    scalar2=None, op0=ALU.bitwise_and,
+                )
+            elif step == 4:
+                nc.vector.tensor_copy(out=small("mp", b, [P, NCH, 3], BF16)[:, :, 0], in_=rows[("nm", b)][:])
+            elif step == 5:
+                nc.vector.tensor_copy(out=small("hl", b, [P, 2, NCH])[:], in_=rows[("hl_i", b)][:])
+            elif step == 6:
+                nc.vector.tensor_tensor(
+                    out=small("r1", b, [P, NCH])[:], in0=rows[("nm", b)][:], in1=rows[("mp", b)][:, :, 0],
+                    op=ALU.subtract,
+                )
+            elif step == 7:
+                nc.vector.tensor_tensor(
+                    out=rows[("mp", b)][:, :, 1], in0=rows[("nm", b)][:], in1=rows[("mp", b)][:, :, 0],
+                    op=ALU.subtract,
+                )
+            elif step == 8:
+                nc.vector.tensor_tensor(
+                    out=small("oh_lo", b, [P, NCH, NCH], BF16)[:],
+                    in0=rev_lo[:].unsqueeze(1).to_broadcast([P, NCH, NCH]),
+                    in1=rows[("hl", b)][:, 1, :].unsqueeze(2).to_broadcast([P, NCH, NCH]),
+                    op=ALU.is_equal,
+                )
+            elif step == 9:
+                nc.vector.tensor_tensor(
+                    out=rows[("mp", b)][:, :, 2], in0=rows[("r1", b)][:], in1=rows[("mp", b)][:, :, 1],
+                    op=ALU.subtract,
+                )
+            elif step == 10:
+                oh = tpool.tile([P, NCH, P], BF16, name="oh", tag="oh")
+                rows[("oh", b)] = oh
+                for c in range(NCH):
+                    nc.vector.tensor_scalar(
+                        out=oh[:, c, :], in0=rev_hi[:], scalar1=rows[("hl", b)][:, 0, c : c + 1],
+                        scalar2=None, op0=ALU.is_equal,
+                    )
+            else:
+                nc.vector.tensor_tensor(
+                    out=small("moh", b, [P, NCH, 3, NCH], BF16)[:],
+                    in0=rows[("oh_lo", b)][:].unsqueeze(2).to_broadcast([P, NCH, 3, NCH]),
+                    in1=rows[("mp", b)][:].unsqueeze(3).to_broadcast([P, NCH, 3, NCH]),
+                    op=ALU.mult,
+                )
+
+        def max_pe(b):
+            mx = ps_small.tile([P, 3 * NCH], F32, name="mx", tag="small")
+            for c in range(NCH):
+                nc.tensor.matmul(
+                    mx[:], lhsT=rows[("oh", b)][:, c, :],
+                    rhs=rows[("moh", b)][:, c, :, :].rearrange("p t a -> p (t a)"),
+                    start=(c == 0), stop=(c == NCH - 1),
+                )
+            rows[("mx", b)] = mx
+
+        def max_v(b):
+            nc.vector.tensor_reduce(
+                out=small("negm", b, [P, NCH])[:], in_=rows[("mx", b)][:].rearrange("p (t a) -> p a t", t=3),
+                axis=AX.X, op=ALU.add,
             )
-
-        def raw_transposes(u, h):
-            b, a = divmod(u, NCH)
-            rt = rows[("rawt", b, a // 4)]
-            q = P * (a % 4)
-            rp = ps_raw.tile([P, HALF], F32, name="rp", tag="rp")
-            for c4 in range(4):
-                nc.tensor.transpose(rp[:, P * c4 : P * (c4 + 1)], rt[:, 4 * h + c4, q : q + P], ident[:])
-            rows[("rp", u, h)] = rp
 
         def store_rows(view, tile_sb, u):
             b, a = divmod(u, NCH)
@@ -211,41 +318,28 @@ def tile_neuralsort_t_kernel(tc, inp, scores, out_0, out_1, out_2):
             elif a % 2 == 1:
                 nc.sync.dma_start(out=view[b, :, a - 1 : a + 1, :], in_=tile_sb[:])
 
-        def copy_max(u, h):
-            a = u % NCH
-            if a % 2 == 0 and h == 0:
-                rows[("raw", u // 2)] = rowp.tile([P, 2, DIM], F32, name="raw_sb", tag="raw_sb")
-            if h == 0:
-                rows[("mx", u)] = usmall.tile([P, 2], F32, name="mx", tag="mx")
+        def logits(u):
+            b, a = divmod(u, NCH)
+            if a % 2 == 0:
+                rows[("raw", u // 2)] = rawp.tile([P, 2, DIM], F32, name="raw_sb", tag="raw_sb")
             raw_sb = rows[("raw", u // 2)]
-            nc.vector.tensor_scalar(
-                out=raw_sb[:, a % 2, HALF * h : HALF * (h + 1)],
-                in0=rows[("rp", u, h)][:],
-                scalar1=1.0,
-                scalar2=None,
-                op0=ALU.mult,
-                op1=ALU.max,
-                accum_out=rows[("mx", u)][:, h : h + 1],
-            )
-            if h == 1:
-                store_rows(raw_v, raw_sb, u)
-
-        def neg_max(u):
-            mx = rows[("mx", u)]
-            negm = usmall.tile([P, 1], F32, name="negm", tag="negm")
-            NEG_ENGINE(nc).tensor_scalar(
-                out=negm[:], in0=mx[:, 0:1], scalar1=mx[:, 1:2], scalar2=-1.0, op0=ALU.max, op1=ALU.mult
-            )
-            rows[("negm", u)] = negm
+            for h in range(2):
+                nc.vector.scalar_tensor_tensor(
+                    out=raw_sb[:, a % 2, HALF * h : HALF * (h + 1)],
+                    in0=e_b[b][:, HALF * h : HALF * (h + 1)],
+                    scalar=s_col[:, a : a + 1],
+                    in1=rows[("rb", b, h)][:],
+                    op0=ALU.mult, op1=ALU.subtract,
+                )
+            store_rows(raw_v, raw_sb, u)
 
         def exponent(u):
-            a = u % NCH
-            raw_sb = rows[("raw", u // 2)]
+            b, a = divmod(u, NCH)
             ex = exp_pool.tile([P, DIM], F32, name="ex", tag="ex")
             ssum = usmall.tile([P, 1], F32, name="ssum", tag="ssum")
             nc.scalar.activation(
-                out=ex[:], in_=raw_sb[:, a % 2, :], func=ACT.Exp, bias=rows[("negm", u)][:], scale=1.0,
-                accum_out=ssum[:],
+                out=ex[:], in_=rows[("raw", u // 2)][:, a % 2, :], func=ACT.Exp,
+                bias=rows[("negm", b)][:, a : a + 1], scale=1.0, accum_out=ssum[:],
             )
             rows[("ex", u)] = ex
             rows[("ssum", u)] = ssum
@@ -258,7 +352,7 @@ def tile_neuralsort_t_kernel(tc, inp, scores, out_0, out_1, out_2):
         def normalise(u, engine):
             a = u % NCH
             if a % 2 == 0:
-                rows[("ph", u // 2)] = rowp.tile([P, 2, DIM], F32, name="ph_sb", tag="ph_sb")
+                rows[("ph", u // 2)] = php.tile([P, 2, DIM], F32, name="ph_sb", tag="ph_sb")
             ph_sb = rows[("ph", u // 2)]
             if engine == "G":
                 nc.gpsimd.tensor_scalar(
@@ -284,14 +378,11 @@ def tile_neuralsort_t_kernel(tc, inp, scores, out_0, out_1, out_2):
         def cast(u, g, engine):
             if ("grp", u) not in rows:
                 rows[("grp", u)] = gpool.tile([P, 2, P, 4], BF16, name="grp", tag="grp", align_bytes=64)
+            src = rows[("pt", u, g)][:].rearrange("p t j -> p j t")
             if engine == "V":
-                nc.vector.tensor_copy(
-                    out=rows[("grp", u)][:, g, :, :], in_=rows[("pt", u, g)][:].rearrange("p t j -> p j t")
-                )
+                nc.vector.tensor_copy(out=rows[("grp", u)][:, g, :, :], in_=src)
             else:
-                nc.scalar.copy(
-                    out=rows[("grp", u)][:, g, :, :], in_=rows[("pt", u, g)][:].rearrange("p t j -> p j t")
-                )
+                nc.scalar.copy(out=rows[("grp", u)][:, g, :, :], in_=src)
 
         def quantise(u):
             codes = gpool.tile([P, 2 * P], U32, name="codes", tag="codes", align_bytes=64)
@@ -302,11 +393,11 @@ def tile_neuralsort_t_kernel(tc, inp, scores, out_0, out_1, out_2):
             )
             rows[("codes", u)] = (codes, scl)
 
-        def multiply_pair(u):
-            b = u // NCH
+        def multiply(units):
             acc = ps_acc.tile([P, 2, Z], F32, name="acc", tag="acc")
-            for w in range(2):
-                codes, scl = rows[("codes", u - 1 + w)]
+            for w, u in enumerate(units):
+                b = u // NCH
+                codes, scl = rows[("codes", u)]
                 for g in range(2):
                     lo = Z * (2 * b + g)
                     nc.tensor.matmul_mx(
@@ -315,204 +406,118 @@ def tile_neuralsort_t_kernel(tc, inp, scores, out_0, out_1, out_2):
                         lhsT_scale=scl[:, P * g : P * (g + 1)],
                         rhs=icodes[:, lo : lo + Z].bitcast(FP8X4),
                         rhs_scale=iscl[:, lo : lo + Z],
-                        start=(g == 0),
-                        stop=(g == 1),
+                        start=(g == 0), stop=(g == 1),
                     )
-            rows[("acc", u)] = acc
+            rows[("acc", units[-1])] = acc
 
-        def multiply_one(u):
-            b = u // NCH
-            acc = ps_acc.tile([P, 2, Z], F32, name="acc", tag="acc")
-            codes, scl = rows[("codes", u)]
-            for g in range(2):
-                lo = Z * (2 * b + g)
-                nc.tensor.matmul_mx(
-                    out=acc[:, 0, :],
-                    lhsT=codes[:, P * g : P * (g + 1)].bitcast(FP8X4),
-                    lhsT_scale=scl[:, P * g : P * (g + 1)],
-                    rhs=icodes[:, lo : lo + Z].bitcast(FP8X4),
-                    rhs_scale=iscl[:, lo : lo + Z],
-                    start=(g == 0),
-                    stop=(g == 1),
-                )
-            rows[("acc", u)] = acc
-
-        def out_one(u, engine):
-            b, a = divmod(u, NCH)
-            out_sb = rows[("out", b)]
-            if engine == "V":
-                nc.vector.tensor_copy(out=out_sb[:, a, :], in_=rows[("acc", u)][:, 0, :])
-            else:
-                nc.scalar.copy(out=out_sb[:, a, :], in_=rows[("acc", u)][:, 0, :])
-            nc.sync.dma_start(out=out_v[b, :, a, :], in_=out_sb[:, a, :])
-
-        def out_pair(u):
-            b, a = divmod(u, NCH)
-            if a == 1:
+        def out_rows(units, engine):
+            b, a = divmod(units[0], NCH)
+            n = len(units)
+            if ("out", b) not in rows:
                 rows[("out", b)] = outp.tile([P, NCH, Z], F32, name="out_sb", tag="out_sb")
             out_sb = rows[("out", b)]
-            nc.scalar.copy(out=out_sb[:, a - 1 : a + 1, :], in_=rows[("acc", u)][:])
-            if b == B - 1 and a >= 5:
-                nc.sync.dma_start(out=out_v[b, :, a - 1 : a + 1, :], in_=out_sb[:, a - 1 : a + 1, :])
-            elif a % 4 == 3:
-                nc.sync.dma_start(out=out_v[b, :, a - 3 : a + 1, :], in_=out_sb[:, a - 3 : a + 1, :])
+            src = rows[("acc", units[-1])][:, 0:n, :]
+            if engine == "V":
+                nc.vector.tensor_copy(out=out_sb[:, a : a + n, :], in_=src)
+            else:
+                nc.scalar.copy(out=out_sb[:, a : a + n, :], in_=src)
+            last = a + n
+            if b == B - 1 and last > 4:
+                nc.sync.dma_start(out=out_v[b, :, a:last, :], in_=out_sb[:, a:last, :])
+            elif last % 4 == 0:
+                nc.sync.dma_start(out=out_v[b, :, last - 4 : last, :], in_=out_sb[:, last - 4 : last, :])
 
-        for b in range(B):
-            spread_scores(b)
         split_e(0)
         split_e(1)
-        compare_v(0, 0)
+        tie_v(0)
         split_e(2)
-        compare_v(0, 1)
+        compare_v(0, 0)
         split_e(3)
+        compare_v(0, 1)
+        total_pe()
+        total_v()
         compare_v(0, 2)
         for ca in range(3):
             compare_pe(0, ca)
         for ca in range(3, NCH):
             compare_v(0, ca)
             compare_pe(0, ca)
-        for b in range(B):
+        tie_pe(0)
+        spread_e(0)
+        spread_e(1)
+        for g in range(2):
+            regroup_input(0, g, "S")
+        spread_e(2)
+        spread_e(3)
+        for b in range(1, B):
             for g in range(2):
-                regroup_input(b, g)
-        compare_v(1, 0)
-        compare_v(1, 1)
-        rowsum(0, 0)
-        rowsum(0, 1)
-        compare_v(1, 2)
-        compare_v(1, 3)
-        rowsum(0, 2)
-        rowsum(0, 3)
-        compare_v(1, 4)
-        compare_v(1, 5)
-        rowsum(0, 4)
-        compare_v(1, 6)
-        compare_v(1, 7)
-        for c in range(NCH):
-            rawt(0, 0, P, c)
-        raw_transposes(0, 0)
-        raw_transposes(0, 1)
-        for c in range(NCH):
-            rawt(0, P, 2 * P, c)
-        raw_transposes(1, 0)
-        raw_transposes(1, 1)
-        for ca in range(NCH):
-            compare_pe(1, ca)
+                regroup_input(b, g, "G")
+        for step in range(5):
+            rowsum(0, step)
+        spread_rowsum(0)
+        for step in range(4):
+            rank(0, step)
+        logits(0)
+        for step in range(4, 12):
+            rank(0, step)
+        max_pe(0)
+        logits(1)
+        max_v(0)
 
-        queue = []
-        pending = []
-        need = {}
-
-        def mark(b, lo, hi):
-            for a in range(lo // P, hi // P):
-                need[NCH * b + a] = len(queue)
-
-        def push_rawt(b, lo, hi):
-            for c in range(NCH):
-                queue.append(("rawt", b, lo, hi, c))
-            mark(b, lo, hi)
-
-        def push_woven(b):
-            for c in range(NCH):
-                if c in (2, 4):
-                    queue.append(("rowsum", b, c - 2))
-                    queue.append(("rowsum", b, c - 1))
-                if c == 6:
-                    queue.append(("rowsum", b, 4))
-                queue.append(("rawt", b - 1, HALF, DIM, c))
-            mark(b - 1, HALF, DIM)
-
-        push_rawt(0, 2 * P, HALF)
-        push_woven(1)
-        push_rawt(1, 0, HALF)
-        for b in range(2, B):
-            for ca in range(NCH):
-                queue.append(("cmp", b, ca))
-            push_woven(b)
-            push_rawt(b, 0, HALF)
-        push_rawt(B - 1, HALF, DIM)
-        done = [0]
-        sent = [0]
-
-        def target(k):
-            if k <= 2:
-                return 8 + 7 * k
-            return 22 + (18 * (k - 2) + 4) // 5
-
-        def fill(k, many):
-            goal = min(len(queue), max(target(k), need.get(k + 2, 0)))
-            while done[0] < goal:
-                item = queue[done[0]]
-                if item[0] == "rowsum" and item[2] == 0 and sent[0] < len(pending):
-                    break
-                done[0] += 1
-                if item[0] == "rawt":
-                    rawt(item[1], item[2], item[3], item[4])
-                elif item[0] == "cmp":
-                    compare_v(item[1], item[2])
-                    pending.append((item[1], item[2]))
-                else:
-                    rowsum(item[1], item[2])
-                if not many:
-                    break
+        def chain(b, a):
+            first = 2 if b == 1 else 0
+            if a < first:
+                return
+            if a == first:
+                tie_v(b)
+                for ca in range(2 * first + 1):
+                    compare_v(b, ca)
+                    compare_pe(b, ca)
+            elif a < 5:
+                for ca in range(2 * a - 1 if a < 4 else 7, min(2 * a + 1, NCH)):
+                    compare_v(b, ca)
+                    compare_pe(b, ca)
+                if a == 4:
+                    tie_pe(b)
+            elif a == 5:
+                for step in range(5):
+                    rowsum(b, step)
+            elif a == 6:
+                for step in range(8):
+                    rank(b, step)
+            else:
+                for step in range(8, 12):
+                    rank(b, step)
+                max_pe(b)
 
         def live(u):
             return 0 <= u < UNITS
 
-        def e_engine(u):
-            return "G" if (E_ON_G and u < UNITS - 2) else "V"
-
-        def cast_on_v(u):
-            return u >= TAIL
-
-        for k in range(UNITS + 10):
+        for k in range(UNITS + 6):
+            if live(k - 1):
+                recip(k - 1)
+                normalise(k - 1, "G" if k - 1 < UNITS - 2 else "V")
+            if live(k - 4) and (k - 4) % 2 == 1:
+                multiply([k - 5, k - 4])
+            if k < UNITS:
+                exponent(k)
+            u = k + AHEAD
+            if live(u) and u % NCH == 0:
+                spread_rowsum(u // NCH)
+                max_v(u // NCH)
             if live(k - 2):
-                recip(k - 2)
-                if e_engine(k - 2) == "G":
-                    normalise(k - 2, "G")
-            if live(k):
-                copy_max(k, 0)
-                copy_max(k, 1)
-                neg_max(k)
-            if live(k - 5):
-                quantise(k - 5)
-            fill(k, False)
-            if live(k - 2) and e_engine(k - 2) == "V":
-                normalise(k - 2, "V")
-            fill(k, True)
-            if live(k - 4) and cast_on_v(k - 4):
-                cast(k - 4, 1, "V")
-            if k == 1:
-                quantise_input(0)
-            if k == 3:
-                quantise_input(1)
-            if k in (12, 20):
-                quantise_input(k // 8 + 1)
-            if k - 1 >= TAIL and live(k - 1):
-                exponent(k - 1)
-            if live(k - 4):
-                cast(k - 4, 0, "S")
-                if not cast_on_v(k - 4):
-                    cast(k - 4, 1, "S")
-            if k - 1 < TAIL and live(k - 1):
-                exponent(k - 1)
-            if live(k - 7) and (k - 7) % 2 == 1 and k - 7 != UNITS - 1:
-                out_pair(k - 7)
-            if live(k + 1) and k + 1 != 1:
-                raw_transposes(k + 1, 0)
-                raw_transposes(k + 1, 1)
+                cast(k - 2, 0, "S")
+                cast(k - 2, 1, "V" if k - 2 >= V_CASTS_FROM else "S")
             if live(k - 3):
-                p_transposes(k - 3, 0)
-                p_transposes(k - 3, 1)
-            if live(k - 6) and (k - 6) % 2 == 1 and k - 6 != UNITS - 1:
-                multiply_pair(k - 6)
-            if k - 6 == UNITS - 2:
-                multiply_one(UNITS - 2)
-            if k - 6 == UNITS - 1:
-                out_one(UNITS - 2, "S")
-                multiply_one(UNITS - 1)
-            if k - 7 == UNITS - 1:
-                out_one(UNITS - 1, "V")
-            while sent[0] < len(pending):
-                compare_pe(pending[sent[0]][0], pending[sent[0]][1])
-                sent[0] += 1
-        assert done[0] == len(queue)
+                quantise(k - 3)
+            if k % NCH == 1 and k < UNITS:
+                quantise_input(k // NCH)
+            if live(u):
+                logits(u)
+            if live(k - 1):
+                p_transposes(k - 1, 0)
+                p_transposes(k - 1, 1)
+            if live(u) and u // NCH + 1 < B:
+                chain(u // NCH + 1, u % NCH)
+            if live(k - 4) and (k - 4) % 2 == 1:
+                out_rows([k - 5, k - 4], "S")

@@ -134,9 +134,7 @@ def tile_neuralsort_t_kernel(tc, inp, scores, out_0, out_1, out_2):
             if engine == "S":
                 nc.scalar.copy(out=igrp[:, 2 * b + g, :, :], in_=src)
             else:
-                nc.gpsimd.tensor_scalar(
-                    out=igrp[:, 2 * b + g, :, :], in0=src, scalar1=1.0, scalar2=0.0, op0=ALU.mult, op1=ALU.add
-                )
+                nc.vector.tensor_copy(out=igrp[:, 2 * b + g, :, :], in_=src)
 
         def quantise_input(b):
             nc.vector.quantize_mx(
@@ -443,15 +441,10 @@ def tile_neuralsort_t_kernel(tc, inp, scores, out_0, out_1, out_2):
             compare_v(0, ca)
             compare_pe(0, ca)
         tie_pe(0)
-        spread_e(0)
-        spread_e(1)
-        for g in range(2):
-            regroup_input(0, g, "S")
-        spread_e(2)
-        spread_e(3)
-        for b in range(1, B):
+        for b in range(2):
+            spread_e(b)
             for g in range(2):
-                regroup_input(b, g, "G")
+                regroup_input(b, g, "S")
         for step in range(5):
             rowsum(0, step)
         spread_rowsum(0)
@@ -494,6 +487,7 @@ def tile_neuralsort_t_kernel(tc, inp, scores, out_0, out_1, out_2):
             return 0 <= u < UNITS
 
         for k in range(UNITS + 6):
+            u = k + AHEAD
             if live(k - 1):
                 recip(k - 1)
                 normalise(k - 1, "G" if k - 1 < UNITS - 2 else "V")
@@ -501,23 +495,27 @@ def tile_neuralsort_t_kernel(tc, inp, scores, out_0, out_1, out_2):
                 multiply([k - 5, k - 4])
             if k < UNITS:
                 exponent(k)
-            u = k + AHEAD
-            if live(u) and u % NCH == 0:
-                spread_rowsum(u // NCH)
-                max_v(u // NCH)
+            if live(u):
+                logits(u)
+                if u % NCH == 0:
+                    max_v(u // NCH)
             if live(k - 2):
-                cast(k - 2, 0, "S")
                 cast(k - 2, 1, "V" if k - 2 >= V_CASTS_FROM else "S")
+                cast(k - 2, 0, "S")
             if live(k - 3):
                 quantise(k - 3)
             if k % NCH == 1 and k < UNITS:
                 quantise_input(k // NCH)
-            if live(u):
-                logits(u)
+            if k in (8, 9, 16, 17):
+                regroup_input(k // NCH + 1, k % 2, "V")
+            if k in (4, 12):
+                spread_e(k // NCH + 2)
             if live(k - 1):
-                p_transposes(k - 1, 0)
                 p_transposes(k - 1, 1)
+                p_transposes(k - 1, 0)
             if live(u) and u // NCH + 1 < B:
                 chain(u // NCH + 1, u % NCH)
+                if u % NCH == NCH - 1:
+                    spread_rowsum(u // NCH + 1)
             if live(k - 4) and (k - 4) % 2 == 1:
                 out_rows([k - 5, k - 4], "S")

@@ -143,18 +143,20 @@ def tile_neuralsort_t_kernel(tc, inp, scores, out_0, out_1, out_2):
                 in_=igrp[:, 2 * b : 2 * b + 2, :, :].rearrange("p g z t -> p (g z t)"),
             )
 
-        def tie_v(b):
-            eq = tpool.tile([P, NCH, P], BF16, name="eq", tag="eq")
-            for c in range(NCH):
+        def tie_v(b, quarter):
+            if quarter == 0:
+                rows[("eq", b)] = tpool.tile([P, NCH, P], BF16, name="eq", tag="eq")
+            eq = rows[("eq", b)]
+            for c in range(2 * quarter, 2 * quarter + 2):
                 nc.vector.tensor_scalar(
                     out=eq[:, c, :], in0=scores_b[b][:, P * c : P * (c + 1)],
                     scalar1=score_col[:, NCH * b + c : NCH * b + c + 1], scalar2=None, op0=ALU.is_equal,
                 )
-            nc.gpsimd.affine_select(
-                out=eq[:], in_=eq[:], pattern=[[0, NCH], [-1, P]], compare_op=ALU.is_gt, fill=0.0,
-                base=0, channel_multiplier=1,
-            )
-            rows[("eq", b)] = eq
+            if quarter == 3:
+                nc.gpsimd.affine_select(
+                    out=eq[:], in_=eq[:], pattern=[[0, NCH], [-1, P]], compare_op=ALU.is_gt, fill=0.0,
+                    base=0, channel_multiplier=1,
+                )
 
         def compare_v(b, ca):
             if ca == 0:
@@ -303,7 +305,7 @@ def tile_neuralsort_t_kernel(tc, inp, scores, out_0, out_1, out_2):
                 )
             rows[("mx", b)] = mx
 
-        def max_v(b):
+        def max_v(b, step):
             nc.vector.tensor_reduce(
                 out=small("negm", b, [P, NCH])[:], in_=rows[("mx", b)][:].rearrange("p (t a) -> p a t", t=3),
                 axis=AX.X, op=ALU.add,
@@ -316,20 +318,20 @@ def tile_neuralsort_t_kernel(tc, inp, scores, out_0, out_1, out_2):
             elif a % 2 == 1:
                 nc.sync.dma_start(out=view[b, :, a - 1 : a + 1, :], in_=tile_sb[:])
 
-        def logits(u):
+        def logits(u, h):
             b, a = divmod(u, NCH)
-            if a % 2 == 0:
+            if a % 2 == 0 and h == 0:
                 rows[("raw", u // 2)] = rawp.tile([P, 2, DIM], F32, name="raw_sb", tag="raw_sb")
             raw_sb = rows[("raw", u // 2)]
-            for h in range(2):
-                nc.vector.scalar_tensor_tensor(
-                    out=raw_sb[:, a % 2, HALF * h : HALF * (h + 1)],
-                    in0=e_b[b][:, HALF * h : HALF * (h + 1)],
-                    scalar=s_col[:, a : a + 1],
-                    in1=rows[("rb", b, h)][:],
-                    op0=ALU.mult, op1=ALU.subtract,
-                )
-            store_rows(raw_v, raw_sb, u)
+            nc.vector.scalar_tensor_tensor(
+                out=raw_sb[:, a % 2, HALF * h : HALF * (h + 1)],
+                in0=e_b[b][:, HALF * h : HALF * (h + 1)],
+                scalar=s_col[:, a : a + 1],
+                in1=rows[("rb", b, h)][:],
+                op0=ALU.mult, op1=ALU.subtract,
+            )
+            if h == 1:
+                store_rows(raw_v, raw_sb, u)
 
         def exponent(u):
             b, a = divmod(u, NCH)
@@ -427,7 +429,8 @@ def tile_neuralsort_t_kernel(tc, inp, scores, out_0, out_1, out_2):
 
         split_e(0)
         split_e(1)
-        tie_v(0)
+        for n in range(4):
+            tie_v(0, n)
         split_e(2)
         compare_v(0, 0)
         split_e(3)
@@ -445,43 +448,56 @@ def tile_neuralsort_t_kernel(tc, inp, scores, out_0, out_1, out_2):
             spread_e(b)
             for g in range(2):
                 regroup_input(b, g, "S")
-        for step in range(5):
-            rowsum(0, step)
+        spread_e(2)
+        spread_e(3)
+        groups = (
+            (rowsum, (0, 1)), (rowsum, (2, 3)), (rowsum, (4,)),
+            (rank, (0, 1)), (rank, (2, 3, 4)), (rank, (5, 6, 7)), (rank, (8, 9, 10)), (rank, (11,)),
+        )
+        queue = []
+        done = [0]
+
+        def gap():
+            if done[0] < len(queue):
+                step_of, b, steps = queue[done[0]]
+                done[0] += 1
+                for step in steps:
+                    step_of(b, step)
+
+        def push_chain(b):
+            for step_of, steps in groups:
+                queue.append((step_of, b, steps))
+
+        push_chain(0)
+        for n in range(3):
+            gap()
+            tie_v(1, n)
         spread_rowsum(0)
-        for step in range(4):
-            rank(0, step)
-        logits(0)
-        for step in range(4, 12):
-            rank(0, step)
+        for u in range(2):
+            for h in range(2):
+                logits(u, h)
+                gap()
+        tie_v(1, 3)
+        gap()
         max_pe(0)
-        logits(1)
-        max_v(0)
+        compare_v(1, 0)
+        compare_pe(1, 0)
+        max_v(0, 0)
 
         def chain(b, a):
-            first = 2 if b == 1 else 0
-            if a < first:
-                return
-            if a == first:
-                tie_v(b)
-                for ca in range(2 * first + 1):
-                    compare_v(b, ca)
-                    compare_pe(b, ca)
-            elif a < 5:
-                for ca in range(2 * a - 1 if a < 4 else 7, min(2 * a + 1, NCH)):
-                    compare_v(b, ca)
-                    compare_pe(b, ca)
-                if a == 4:
-                    tie_pe(b)
-            elif a == 5:
-                for step in range(5):
-                    rowsum(b, step)
-            elif a == 6:
-                for step in range(8):
-                    rank(b, step)
+            if b == 1:
+                chunks = {2: (1, 2), 3: (3, 4, 5), 4: (6, 7)}
             else:
-                for step in range(8, 12):
-                    rank(b, step)
-                max_pe(b)
+                chunks = {0: (0,), 1: (1, 2), 2: (3, 4), 3: (5, 6), 4: (7,)}
+                if a == 0:
+                    for n in range(4):
+                        tie_v(b, n)
+            for ca in chunks.get(a, ()):
+                compare_v(b, ca)
+                compare_pe(b, ca)
+            if a == 4:
+                tie_pe(b)
+                push_chain(b)
 
         def live(u):
             return 0 <= u < UNITS
@@ -496,26 +512,29 @@ def tile_neuralsort_t_kernel(tc, inp, scores, out_0, out_1, out_2):
             if k < UNITS:
                 exponent(k)
             if live(u):
-                logits(u)
-                if u % NCH == 0:
-                    max_v(u // NCH)
+                for h in range(2):
+                    logits(u, h)
+                    gap()
+                if u % NCH == NCH - 1 and u // NCH + 1 < B:
+                    spread_rowsum(u // NCH + 1)
             if live(k - 2):
                 cast(k - 2, 1, "V" if k - 2 >= V_CASTS_FROM else "S")
                 cast(k - 2, 0, "S")
             if live(k - 3):
                 quantise(k - 3)
+                gap()
             if k % NCH == 1 and k < UNITS:
                 quantise_input(k // NCH)
             if k in (8, 9, 16, 17):
                 regroup_input(k // NCH + 1, k % 2, "V")
-            if k in (4, 12):
-                spread_e(k // NCH + 2)
             if live(k - 1):
                 p_transposes(k - 1, 1)
                 p_transposes(k - 1, 0)
             if live(u) and u // NCH + 1 < B:
                 chain(u // NCH + 1, u % NCH)
                 if u % NCH == NCH - 1:
-                    spread_rowsum(u // NCH + 1)
+                    max_pe(u // NCH + 1)
+                    queue.append((max_v, u // NCH + 1, (0,)))
             if live(k - 4) and (k - 4) % 2 == 1:
                 out_rows([k - 5, k - 4], "S")
+        assert done[0] == len(queue)

@@ -21,6 +21,9 @@ UNITS = B * NCH
 FLOPS = 2 * B * DIM * DIM * Z
 AHEAD = 2
 V_CASTS_FROM = 22
+CAST_LAG = 3
+QUANT_LAG = 5
+V_OUT_FROM = 24
 
 
 def tile_neuralsort_t_kernel(tc, inp, scores, out_0, out_1, out_2):
@@ -37,10 +40,10 @@ def tile_neuralsort_t_kernel(tc, inp, scores, out_0, out_1, out_2):
         rawp = ctx.enter_context(tc.tile_pool(name="rawp", bufs=5))
         php = ctx.enter_context(tc.tile_pool(name="php", bufs=3))
         exp_pool = ctx.enter_context(tc.tile_pool(name="exp_pool", bufs=3))
-        gpool = ctx.enter_context(tc.tile_pool(name="gpool", bufs=4))
+        gpool = ctx.enter_context(tc.tile_pool(name="gpool", bufs=6))
         outp = ctx.enter_context(tc.tile_pool(name="outp", bufs=2))
         bsmall = ctx.enter_context(tc.tile_pool(name="bsmall", bufs=2))
-        usmall = ctx.enter_context(tc.tile_pool(name="usmall", bufs=4))
+        usmall = ctx.enter_context(tc.tile_pool(name="usmall", bufs=6))
         ps_rb = ctx.enter_context(tc.psum_pool(name="ps_rb", bufs=1))
         ps_pt = ctx.enter_context(tc.psum_pool(name="ps_pt", bufs=4))
         ps_acc = ctx.enter_context(tc.psum_pool(name="ps_acc", bufs=1))
@@ -77,6 +80,12 @@ def tile_neuralsort_t_kernel(tc, inp, scores, out_0, out_1, out_2):
         rev_lo = const.tile([P, NCH], F32, name="rev_lo", tag="rev_lo")
         nc.gpsimd.iota(
             rev_lo[:], pattern=[[-1, NCH]], base=NCH - 1, channel_multiplier=0, allow_small_or_imprecise_dtypes=True
+        )
+        margin = const.tile([P, P], F32, name="margin", tag="margin")
+        nc.gpsimd.memset(margin[:], -(2.0 ** -126))
+        nc.gpsimd.affine_select(
+            out=margin[:], in_=margin[:], pattern=[[-1, P]], compare_op=ALU.is_gt, fill=0.0,
+            base=0, channel_multiplier=1,
         )
         ones_bf = const.tile([P, P], BF16, name="ones_bf", tag="ones_bf")
         nc.vector.memset(ones_bf[:], 1.0)
@@ -143,88 +152,71 @@ def tile_neuralsort_t_kernel(tc, inp, scores, out_0, out_1, out_2):
                 in_=igrp[:, 2 * b : 2 * b + 2, :, :].rearrange("p g z t -> p (g z t)"),
             )
 
-        def tie_v(b, quarter):
-            if quarter == 0:
-                rows[("eq", b)] = tpool.tile([P, NCH, P], BF16, name="eq", tag="eq")
-            eq = rows[("eq", b)]
-            for c in range(2 * quarter, 2 * quarter + 2):
-                nc.vector.tensor_scalar(
-                    out=eq[:, c, :], in0=scores_b[b][:, P * c : P * (c + 1)],
-                    scalar1=score_col[:, NCH * b + c : NCH * b + c + 1], scalar2=None, op0=ALU.is_equal,
-                )
-            if quarter == 3:
-                nc.gpsimd.affine_select(
-                    out=eq[:], in_=eq[:], pattern=[[0, NCH], [-1, P]], compare_op=ALU.is_gt, fill=0.0,
-                    base=0, channel_multiplier=1,
-                )
-
-        def compare_v(b, ca):
-            if ca == 0:
+        def compare_v(b, ca, h):
+            if ca == 0 and h == 0:
                 rows[("cmp", b)] = tpool.tile([P, NCH, DIM], BF16, name="cmp", tag="cmp")
             cmp = rows[("cmp", b)]
-            col = NCH * b + ca
-            if ca:
+            score = score_col[:, NCH * b + ca : NCH * b + ca + 1]
+            lo, hi = HALF * h, HALF * (h + 1)
+            d0, d1 = min(max(P * ca, lo), hi), min(max(P * (ca + 1), lo), hi)
+            if d0 > lo:
                 nc.vector.tensor_scalar(
-                    out=cmp[:, ca, 0 : P * ca], in0=scores_b[b][:, 0 : P * ca],
-                    scalar1=score_col[:, col : col + 1], scalar2=None, op0=ALU.is_ge,
+                    out=cmp[:, ca, lo:d0], in0=scores_b[b][:, lo:d0], scalar1=score, scalar2=None, op0=ALU.is_ge
                 )
-            nc.vector.tensor_scalar(
-                out=cmp[:, ca, P * ca : DIM], in0=scores_b[b][:, P * ca : DIM],
-                scalar1=score_col[:, col : col + 1], scalar2=None, op0=ALU.is_gt,
-            )
-
-        def compare_pe(b, ca):
-            if ca == 0:
-                rows[("ls", b)] = ps_small.tile([P, NCH, NCH + 1, 4], F32, name="ls", tag="small")
-            ls = rows[("ls", b)]
-            cmp = rows[("cmp", b)]
-            for cb in range(NCH):
-                nc.tensor.matmul(
-                    ls[:, cb, ca, :], lhsT=cmp[:, ca, P * cb : P * (cb + 1)], rhs=parts[:, NCH * b + ca, :],
-                    start=True, stop=True,
+            if d1 > d0:
+                nc.vector.scalar_tensor_tensor(
+                    out=cmp[:, ca, d0:d1], in0=scores_b[b][:, d0:d1], scalar=score, in1=margin[:],
+                    op0=ALU.subtract, op1=ALU.is_gt,
+                )
+            if hi > d1:
+                nc.vector.tensor_scalar(
+                    out=cmp[:, ca, d1:hi], in0=scores_b[b][:, d1:hi], scalar1=score, scalar2=None, op0=ALU.is_gt
                 )
 
-        def tie_pe(b):
+        def compare_pe(b, ca, h):
+            if ca == 0 and h == 0:
+                if b == 0:
+                    rows["sums"] = ps_small.tile([P, 2, 4 * NCH * NCH], F32, name="sums", tag="small")
+                sums = rows["sums"][:, b % 2, :]
+                rows[("ls", b)] = sums.rearrange("p (c k t) -> p c k t", c=NCH, t=4)
+                rows[("mx", b)] = sums[:, 0 : 2 * NCH]
             ls = rows[("ls", b)]
-            for c in range(NCH):
+            for cb in range(4 * h, 4 * h + 4):
                 nc.tensor.matmul(
-                    ls[:, c, NCH, :], lhsT=rows[("eq", b)][:, c, :], rhs=parts[:, NCH * b + c, :],
-                    start=True, stop=True,
+                    ls[:, cb, ca, :], lhsT=rows[("cmp", b)][:, ca, P * cb : P * (cb + 1)],
+                    rhs=parts[:, NCH * b + ca, :], start=True, stop=True,
                 )
 
         def small(key, b, shape, dtype=F32):
-            t = bsmall.tile(shape, dtype, name=key, tag=key)
-            rows[(key, b)] = t
-            return t
+            if (key, b) not in rows:
+                rows[(key, b)] = bsmall.tile(shape, dtype, name=key, tag=key)
+            return rows[(key, b)]
 
-        def rowsum(b, step):
+        def rowsum(b, step, c0=0, c1=NCH):
             ls = rows[("ls", b)]
-            e = e_col[:, NCH * b : NCH * (b + 1)]
+            e = e_col[:, NCH * b + c0 : NCH * b + c1]
+            cnt, below = small("cnt", b, [P, NCH]), small("below", b, [P, NCH])
+            x1, x2 = small("x1", b, [P, NCH]), small("x2", b, [P, NCH])
             if step == 0:
-                nc.vector.tensor_reduce(
-                    out=small("cnt", b, [P, NCH])[:], in_=ls[:, :, :, 0], axis=AX.X, op=ALU.add
-                )
+                nc.vector.tensor_reduce(out=cnt[:, c0:c1], in_=ls[:, c0:c1, :, 0], axis=AX.X, op=ALU.add)
             elif step == 1:
-                nc.vector.tensor_reduce(
-                    out=small("below", b, [P, NCH])[:], in_=ls[:, :, :, 1:4], axis=AX.XY, op=ALU.add
-                )
+                nc.vector.tensor_reduce(out=below[:, c0:c1], in_=ls[:, c0:c1, :, 1:4], axis=AX.XY, op=ALU.add)
             elif step == 2:
                 nc.vector.scalar_tensor_tensor(
-                    out=small("x1", b, [P, NCH])[:], in0=rows[("cnt", b)][:], scalar=2.0, in1=e,
-                    op0=ALU.mult, op1=ALU.mult,
+                    out=x1[:, c0:c1], in0=cnt[:, c0:c1], scalar=2.0, in1=e, op0=ALU.mult, op1=ALU.mult
                 )
             elif step == 3:
                 nc.vector.tensor_scalar(
-                    out=small("x2", b, [P, NCH])[:], in0=rows[("below", b)][:], scalar1=-2.0,
-                    scalar2=t_all[:, b : b + 1], op0=ALU.mult, op1=ALU.add,
+                    out=x2[:, c0:c1], in0=below[:, c0:c1], scalar1=-2.0, scalar2=t_all[:, b : b + 1],
+                    op0=ALU.mult, op1=ALU.add,
                 )
             else:
                 nc.vector.tensor_tensor(
-                    out=small("rsum", b, [P, NCH])[:], in0=rows[("x1", b)][:], in1=rows[("x2", b)][:], op=ALU.add
+                    out=small("rsum", b, [P, NCH])[:, c0:c1], in0=x1[:, c0:c1], in1=x2[:, c0:c1], op=ALU.add
                 )
 
-        def spread_rowsum(b):
-            for h in range(2):
+        def spread_rowsum(b, halves=(0, 1)):
+            for h in halves:
                 rb = ps_rb.tile([P, HALF], F32, name="rb%d" % h, tag="rb%d" % h)
                 for c in range(4):
                     col = 4 * h + c
@@ -240,8 +232,8 @@ def tile_neuralsort_t_kernel(tc, inp, scores, out_0, out_1, out_2):
                 nc.vector.tensor_copy(out=small("cnt_i", b, [P, NCH], I32)[:], in_=rows[("cnt", b)][:])
             elif step == 1:
                 nc.vector.tensor_tensor(
-                    out=small("nm", b, [P, NCH])[:], in0=rows[("x2", b)][:], in1=e_col[:, NCH * b : NCH * (b + 1)],
-                    op=ALU.subtract,
+                    out=small("nm", b, [P, NCH])[:], in0=rows[("x2", b)][:],
+                    in1=e_col[:, NCH * b : NCH * (b + 1)], op=ALU.subtract,
                 )
             elif step == 2:
                 nc.vector.tensor_scalar(
@@ -253,33 +245,23 @@ def tile_neuralsort_t_kernel(tc, inp, scores, out_0, out_1, out_2):
                     out=rows[("hl_i", b)][:, 1, :], in0=rows[("cnt_i", b)][:], scalar1=7,
                     scalar2=None, op0=ALU.bitwise_and,
                 )
-            elif step == 4:
-                nc.vector.tensor_copy(out=small("mp", b, [P, NCH, 3], BF16)[:, :, 0], in_=rows[("nm", b)][:])
             elif step == 5:
                 nc.vector.tensor_copy(out=small("hl", b, [P, 2, NCH])[:], in_=rows[("hl_i", b)][:])
-            elif step == 6:
-                nc.vector.tensor_tensor(
-                    out=small("r1", b, [P, NCH])[:], in0=rows[("nm", b)][:], in1=rows[("mp", b)][:, :, 0],
-                    op=ALU.subtract,
-                )
+            elif step == 4:
+                nc.vector.tensor_copy(out=small("mp", b, [P, NCH, 2], BF16)[:, :, 0], in_=rows[("nm", b)][:])
             elif step == 7:
-                nc.vector.tensor_tensor(
-                    out=rows[("mp", b)][:, :, 1], in0=rows[("nm", b)][:], in1=rows[("mp", b)][:, :, 0],
-                    op=ALU.subtract,
-                )
-            elif step == 8:
                 nc.vector.tensor_tensor(
                     out=small("oh_lo", b, [P, NCH, NCH], BF16)[:],
                     in0=rev_lo[:].unsqueeze(1).to_broadcast([P, NCH, NCH]),
                     in1=rows[("hl", b)][:, 1, :].unsqueeze(2).to_broadcast([P, NCH, NCH]),
                     op=ALU.is_equal,
                 )
-            elif step == 9:
+            elif step == 6:
                 nc.vector.tensor_tensor(
-                    out=rows[("mp", b)][:, :, 2], in0=rows[("r1", b)][:], in1=rows[("mp", b)][:, :, 1],
+                    out=rows[("mp", b)][:, :, 1], in0=rows[("nm", b)][:], in1=rows[("mp", b)][:, :, 0],
                     op=ALU.subtract,
                 )
-            elif step == 10:
+            elif step == 8:
                 oh = tpool.tile([P, NCH, P], BF16, name="oh", tag="oh")
                 rows[("oh", b)] = oh
                 for c in range(NCH):
@@ -289,25 +271,23 @@ def tile_neuralsort_t_kernel(tc, inp, scores, out_0, out_1, out_2):
                     )
             else:
                 nc.vector.tensor_tensor(
-                    out=small("moh", b, [P, NCH, 3, NCH], BF16)[:],
-                    in0=rows[("oh_lo", b)][:].unsqueeze(2).to_broadcast([P, NCH, 3, NCH]),
-                    in1=rows[("mp", b)][:].unsqueeze(3).to_broadcast([P, NCH, 3, NCH]),
+                    out=small("moh", b, [P, NCH, 2, NCH], BF16)[:],
+                    in0=rows[("oh_lo", b)][:].unsqueeze(2).to_broadcast([P, NCH, 2, NCH]),
+                    in1=rows[("mp", b)][:].unsqueeze(3).to_broadcast([P, NCH, 2, NCH]),
                     op=ALU.mult,
                 )
 
         def max_pe(b):
-            mx = ps_small.tile([P, 3 * NCH], F32, name="mx", tag="small")
             for c in range(NCH):
                 nc.tensor.matmul(
-                    mx[:], lhsT=rows[("oh", b)][:, c, :],
+                    rows[("mx", b)], lhsT=rows[("oh", b)][:, c, :],
                     rhs=rows[("moh", b)][:, c, :, :].rearrange("p t a -> p (t a)"),
                     start=(c == 0), stop=(c == NCH - 1),
                 )
-            rows[("mx", b)] = mx
 
         def max_v(b, step):
             nc.vector.tensor_reduce(
-                out=small("negm", b, [P, NCH])[:], in_=rows[("mx", b)][:].rearrange("p (t a) -> p a t", t=3),
+                out=small("negm", b, [P, NCH])[:], in_=rows[("mx", b)].rearrange("p (t a) -> p a t", t=2),
                 axis=AX.X, op=ALU.add,
             )
 
@@ -393,8 +373,11 @@ def tile_neuralsort_t_kernel(tc, inp, scores, out_0, out_1, out_2):
             )
             rows[("codes", u)] = (codes, scl)
 
-        def multiply(units):
-            acc = ps_acc.tile([P, 2, Z], F32, name="acc", tag="acc")
+        def multiply(units, late):
+            if late:
+                acc = ps_pt.tile([P, 2, Z], F32, name="acc_late", tag="pt")
+            else:
+                acc = ps_acc.tile([P, 2, Z], F32, name="acc", tag="acc")
             for w, u in enumerate(units):
                 b = u // NCH
                 codes, scl = rows[("codes", u)]
@@ -427,114 +410,163 @@ def tile_neuralsort_t_kernel(tc, inp, scores, out_0, out_1, out_2):
             elif last % 4 == 0:
                 nc.sync.dma_start(out=out_v[b, :, last - 4 : last, :], in_=out_sb[:, last - 4 : last, :])
 
-        split_e(0)
-        split_e(1)
-        for n in range(4):
-            tie_v(0, n)
-        split_e(2)
-        compare_v(0, 0)
-        split_e(3)
-        compare_v(0, 1)
-        total_pe()
+        for h in range(2):
+            for ca in range(NCH):
+                compare_v(0, ca, h)
+                if h == 0 and ca == 2:
+                    for step in range(4):
+                        split_e(step)
+                    total_pe()
+                    for c in range(3):
+                        compare_pe(0, c, h)
+                elif h == 1 or ca > 2:
+                    compare_pe(0, ca, h)
         total_v()
-        compare_v(0, 2)
-        for ca in range(3):
-            compare_pe(0, ca)
-        for ca in range(3, NCH):
-            compare_v(0, ca)
-            compare_pe(0, ca)
-        tie_pe(0)
-        for b in range(2):
-            spread_e(b)
-            for g in range(2):
-                regroup_input(b, g, "S")
+        spread_e(0)
+        spread_e(1)
+        for g in range(2):
+            regroup_input(0, g, "S")
         spread_e(2)
-        spread_e(3)
+        for g in range(2):
+            regroup_input(1, g, "S")
+        for steps in ((0, 1), (2, 3), (4,)):
+            for h in range(2):
+                for step in steps:
+                    rowsum(0, step, 4 * h, 4 * h + 4)
+                if steps == (4,):
+                    spread_rowsum(0, (h,))
+        rank(0, 0)
+        rank(0, 1)
+        compare_v(1, 0, 0)
+        for step in (2, 3, 4):
+            rank(0, step)
+        logits(0, 0)
+        rank(0, 5)
+        rank(0, 6)
+        logits(0, 1)
+        rank(0, 7)
+        rank(0, 8)
+        compare_v(1, 0, 1)
+        rank(0, 9)
+        max_pe(0)
+        compare_v(1, 1, 0)
+        compare_v(1, 1, 1)
+        max_v(0, 0)
+        for n in range(4):
+            compare_pe(1, n // 2, n % 2)
+        logits(1, 0)
+        logits(1, 1)
+
         groups = (
             (rowsum, (0, 1)), (rowsum, (2, 3)), (rowsum, (4,)),
-            (rank, (0, 1)), (rank, (2, 3, 4)), (rank, (5, 6, 7)), (rank, (8, 9, 10)), (rank, (11,)),
+            (rank, (0, 1)), (rank, (2, 3, 4)), (rank, (5, 6)), (rank, (7, 8)), (rank, (9,)), (max_v, (0,)),
         )
         queue = []
+
+        def push_pieces(b, start, stop):
+            for n in range(start, stop):
+                queue.append(("cmp", b, n // 2, n % 2))
+
+        push_pieces(1, 4, 2 * NCH)
+        for b in range(1, B):
+            if b + 1 < B:
+                push_pieces(b + 1, 0, 3)
+            for n in range(len(groups)):
+                queue.append(("group", b, n, 0))
+                if b + 1 < B and n + 3 < 2 * NCH:
+                    push_pieces(b + 1, n + 3, n + 4)
+            if b + 1 < B:
+                push_pieces(b + 1, len(groups) + 3, 2 * NCH)
         done = [0]
+        rb_ready = [0]
 
-        def gap():
-            if done[0] < len(queue):
-                step_of, b, steps = queue[done[0]]
+        def fill(goal):
+            while done[0] < min(goal, len(queue)):
+                kind, b, x, y = queue[done[0]]
                 done[0] += 1
-                for step in steps:
-                    step_of(b, step)
-
-        def push_chain(b):
-            for step_of, steps in groups:
-                queue.append((step_of, b, steps))
-
-        push_chain(0)
-        for n in range(3):
-            gap()
-            tie_v(1, n)
-        spread_rowsum(0)
-        for u in range(2):
-            for h in range(2):
-                logits(u, h)
-                gap()
-        tie_v(1, 3)
-        gap()
-        max_pe(0)
-        compare_v(1, 0)
-        compare_pe(1, 0)
-        max_v(0, 0)
-
-        def chain(b, a):
-            if b == 1:
-                chunks = {2: (1, 2), 3: (3, 4, 5), 4: (6, 7)}
-            else:
-                chunks = {0: (0,), 1: (1, 2), 2: (3, 4), 3: (5, 6), 4: (7,)}
-                if a == 0:
-                    for n in range(4):
-                        tie_v(b, n)
-            for ca in chunks.get(a, ()):
-                compare_v(b, ca)
-                compare_pe(b, ca)
-            if a == 4:
-                tie_pe(b)
-                push_chain(b)
+                if kind == "cmp":
+                    compare_v(b, x, y)
+                    compare_pe(b, x, y)
+                else:
+                    step_of, steps = groups[x]
+                    for step in steps:
+                        step_of(b, step)
+                    if step_of is rowsum and steps == (4,):
+                        rb_ready[0] = b
+                    if step_of is rank and steps == (9,):
+                        max_pe(b)
 
         def live(u):
             return 0 <= u < UNITS
 
-        for k in range(UNITS + 6):
+        per_batch = 2 * NCH + len(groups)
+
+        def goal(k):
+            if k < 4:
+                return 3 * (k + 1)
+            return 23 + per_batch * (k - 4) // NCH
+
+        sent = {}
+
+        def due(stage, limit):
+            first = sent.get(stage, 0)
+            last = min(limit, UNITS - 1)
+            sent[stage] = max(first, last + 1)
+            return range(first, last + 1)
+
+        for k in range(UNITS + 1):
             u = k + AHEAD
-            if live(k - 1):
-                recip(k - 1)
-                normalise(k - 1, "G" if k - 1 < UNITS - 2 else "V")
-            if live(k - 4) and (k - 4) % 2 == 1:
-                multiply([k - 5, k - 4])
+            late = k >= UNITS
+            cast_lag = 1 if late else CAST_LAG
+            quant_lag = 1 if late else (QUANT_LAG - 1 if k >= UNITS - NCH + 2 else QUANT_LAG)
+            if not late:
+                for v in due("multiply", sent.get("quantise", 0) - 1):
+                    if v % 2 == 1:
+                        multiply([v - 1, v], False)
+            if not late:
+                for v in due("transpose", k - cast_lag + 1):
+                    p_transposes(v, 1)
+                    p_transposes(v, 0)
+            for v in due("normalise", k - 1):
+                recip(v)
+                normalise(v, "G" if v < UNITS - 2 else "V")
             if k < UNITS:
                 exponent(k)
+            if not late:
+                for v in due("quantise", k - quant_lag):
+                    quantise(v)
+            if u % NCH == 0:
+                fill(goal(k))
             if live(u):
                 for h in range(2):
                     logits(u, h)
-                    gap()
-                if u % NCH == NCH - 1 and u // NCH + 1 < B:
-                    spread_rowsum(u // NCH + 1)
-            if live(k - 2):
-                cast(k - 2, 1, "V" if k - 2 >= V_CASTS_FROM else "S")
-                cast(k - 2, 0, "S")
-            if live(k - 3):
-                quantise(k - 3)
-                gap()
+            if late:
+                for v in due("transpose", k - 1):
+                    p_transposes(v, 1)
+                    p_transposes(v, 0)
+            for v in due("cast", k - cast_lag):
+                cast(v, 1, "V" if v >= V_CASTS_FROM else "S")
+                cast(v, 0, "S")
             if k % NCH == 1 and k < UNITS:
                 quantise_input(k // NCH)
-            if k in (8, 9, 16, 17):
-                regroup_input(k // NCH + 1, k % 2, "V")
-            if live(k - 1):
-                p_transposes(k - 1, 1)
-                p_transposes(k - 1, 0)
-            if live(u) and u // NCH + 1 < B:
-                chain(u // NCH + 1, u % NCH)
-                if u % NCH == NCH - 1:
-                    max_pe(u // NCH + 1)
-                    queue.append((max_v, u // NCH + 1, (0,)))
-            if live(k - 4) and (k - 4) % 2 == 1:
-                out_rows([k - 5, k - 4], "S")
+            if 2 <= k < 6:
+                regroup_input(k // 2 + 1, k % 2, "S")
+            if k == 12:
+                spread_e(3)
+            fill(goal(k))
+            if u % NCH == NCH - 1 and u // NCH + 1 < B:
+                assert rb_ready[0] == u // NCH + 1
+                spread_rowsum(u // NCH + 1)
+            if late:
+                for v in due("quantise", k - quant_lag):
+                    quantise(v)
+                last = [[v] if v >= UNITS - 2 else [v - 1, v] for v in due("multiply", UNITS) if v >= UNITS - 2 or v % 2]
+                for units in last:
+                    multiply(units, True)
+                for n, units in enumerate(last):
+                    out_rows(units, "SV"[n % 2])
+            else:
+                for v in due("out", sent.get("multiply", 0) - 1):
+                    if v % 2 == 1:
+                        out_rows([v - 1, v], "V" if v >= V_OUT_FROM else "S")
         assert done[0] == len(queue)

@@ -121,7 +121,7 @@ def tile_neuralsort_t_kernel(tc, inp, scores, out_0, out_1, out_2):
                 nc.vector.tensor_tensor(out=parts[:, :, 3], in0=rest1[:], in1=parts[:, :, 2], op=ALU.subtract)
 
         def total_pe():
-            tot = ps_small.tile([P, B * NCH * 4], F32, name="tot", tag="small")
+            tot = ps_pt.tile([P, B * NCH * 4], F32, name="tot", tag="pt")
             nc.tensor.matmul(
                 tot[:], lhsT=ones_bf[:], rhs=parts[:].rearrange("p c t -> p (c t)"), start=True, stop=True
             )
@@ -139,11 +139,12 @@ def tile_neuralsort_t_kernel(tc, inp, scores, out_0, out_1, out_2):
             nc.scalar.activation(out=e_b[b][:], in_=scores_b[b][:], func=ACT.Exp)
 
         def regroup_input(b, g, engine):
-            src = in_raw[b][:, 4 * g : 4 * g + 4, :].rearrange("p t z -> p z t")
+            src = in_raw[b][:, 4 * g : 4 * g + 4, :].rearrange("p t (c i) -> p c t i", i=4)
+            dst = igrp[:, 2 * b + g, :, :].rearrange("p (c i) t -> p c t i", i=4)
             if engine == "S":
-                nc.scalar.copy(out=igrp[:, 2 * b + g, :, :], in_=src)
+                nc.scalar.copy(out=dst, in_=src)
             else:
-                nc.vector.tensor_copy(out=igrp[:, 2 * b + g, :, :], in_=src)
+                nc.vector.tensor_copy(out=dst, in_=src)
 
         def quantise_input(b):
             nc.vector.quantize_mx(
@@ -429,6 +430,7 @@ def tile_neuralsort_t_kernel(tc, inp, scores, out_0, out_1, out_2):
         spread_e(2)
         for g in range(2):
             regroup_input(1, g, "S")
+        spread_e(3)
         for steps in ((0, 1), (2, 3), (4,)):
             for h in range(2):
                 for step in steps:
@@ -551,8 +553,6 @@ def tile_neuralsort_t_kernel(tc, inp, scores, out_0, out_1, out_2):
                 quantise_input(k // NCH)
             if 2 <= k < 6:
                 regroup_input(k // 2 + 1, k % 2, "S")
-            if k == 12:
-                spread_e(3)
             fill(goal(k))
             if u % NCH == NCH - 1 and u // NCH + 1 < B:
                 assert rb_ready[0] == u // NCH + 1

@@ -51,16 +51,15 @@ def tile_neuralsort_t_kernel(tc, inp, scores, out_0, out_1, out_2):
 
         xz = const.tile([P, P], BF16, name="xz", tag="xz")
         nc.sync.dma_start(out=xz[0:32, :], in_=scores.rearrange("b (c p) -> (b c) p", p=P))
-        scores_b = []
-        for b in range(B):
-            sb = const.tile([P, DIM], BF16, name="scores_b%d" % b, tag="scores_b%d" % b)
-            nc.sync.dma_start(out=sb[:], in_=scores[b].partition_broadcast(P))
-            scores_b.append(sb)
-        in_raw = []
-        for b in range(B):
-            ir = const.tile([P, NCH, Z], BF16, name="in_raw%d" % b, tag="in_raw%d" % b)
-            nc.sync.dma_start(out=ir[:], in_=in_v[b])
-            in_raw.append(ir)
+        scores_b = [const.tile([P, DIM], BF16, name="scores_b%d" % b, tag="scores_b%d" % b) for b in range(B)]
+        in_raw = [const.tile([P, NCH, Z], BF16, name="in_raw%d" % b, tag="in_raw%d" % b) for b in range(B)]
+        nc.scalar.dma_start(out=scores_b[0][:], in_=scores[0].partition_broadcast(P))
+        nc.sync.dma_start(out=in_raw[0][:], in_=in_v[0])
+        nc.sync.dma_start(out=scores_b[1][:], in_=scores[1].partition_broadcast(P))
+        for b in range(1, B):
+            nc.sync.dma_start(out=in_raw[b][:], in_=in_v[b])
+        for b in range(2, B):
+            nc.sync.dma_start(out=scores_b[b][:], in_=scores[b].partition_broadcast(P))
 
         nc.vector.memset(xz[32:64, :], 0.0)
         nc.vector.memset(xz[64:128, :], 0.0)
@@ -424,12 +423,12 @@ def tile_neuralsort_t_kernel(tc, inp, scores, out_0, out_1, out_2):
                     compare_pe(0, ca, h)
         total_v()
         spread_e(0)
-        spread_e(1)
         for g in range(2):
             regroup_input(0, g, "S")
-        spread_e(2)
+        spread_e(1)
         for g in range(2):
             regroup_input(1, g, "S")
+        spread_e(2)
         spread_e(3)
         for steps in ((0, 1), (2, 3), (4,)):
             for h in range(2):

@@ -455,8 +455,9 @@ def tile_neuralsort_t_kernel(tc, inp, scores, out_0, out_1, out_2):
         max_v(0, 0)
         for n in range(4):
             compare_pe(1, n // 2, n % 2)
-        logits(1, 0)
-        logits(1, 1)
+        for u in range(1, AHEAD):
+            for h in range(2):
+                logits(u, h)
 
         groups = (
             (rowsum, (0, 1)), (rowsum, (2, 3)), (rowsum, (4,)),
@@ -504,8 +505,8 @@ def tile_neuralsort_t_kernel(tc, inp, scores, out_0, out_1, out_2):
 
         def goal(k):
             if k < 4:
-                return 3 * (k + 1)
-            return 23 + per_batch * (k - 4) // NCH
+                return 4 * (k + 1)
+            return 3 * NCH + per_batch * (k - 4) // NCH
 
         sent = {}
 
@@ -538,6 +539,8 @@ def tile_neuralsort_t_kernel(tc, inp, scores, out_0, out_1, out_2):
                     quantise(v)
             if u % NCH == 0:
                 fill(goal(k))
+            elif k < 5:
+                fill(goal(k) - 1)
             if live(u):
                 for h in range(2):
                     logits(u, h)

@@ -20,7 +20,7 @@ HALF = 512
 UNITS = B * NCH
 FLOPS = 2 * B * DIM * DIM * Z
 AHEAD = 2
-V_CASTS_FROM = 22
+V_CASTS_FROM = 20
 CAST_LAG = 3
 QUANT_LAG = 5
 V_OUT_FROM = 24
@@ -340,10 +340,12 @@ def tile_neuralsort_t_kernel(tc, inp, scores, out_0, out_1, out_2):
                     op0=ALU.mult, op1=ALU.add,
                 )
             else:
-                nc.vector.tensor_scalar(
-                    out=ph_sb[:, a % 2, :], in0=rows[("ex", u)][:], scalar1=rows[("rinv", u)][:], scalar2=None,
-                    op0=ALU.mult,
-                )
+                for h in range(2):
+                    cols = slice(HALF * h, HALF * (h + 1))
+                    nc.vector.tensor_scalar(
+                        out=ph_sb[:, a % 2, cols], in0=rows[("ex", u)][:, cols], scalar1=rows[("rinv", u)][:],
+                        scalar2=None, op0=ALU.mult,
+                    )
             store_rows(ph_v, ph_sb, u)
 
         def p_transposes(u, g):
@@ -516,27 +518,21 @@ def tile_neuralsort_t_kernel(tc, inp, scores, out_0, out_1, out_2):
             sent[stage] = max(first, last + 1)
             return range(first, last + 1)
 
-        for k in range(UNITS + 1):
+        for k in range(UNITS):
             u = k + AHEAD
-            late = k >= UNITS
-            cast_lag = 1 if late else CAST_LAG
-            quant_lag = 1 if late else (QUANT_LAG - 1 if k >= UNITS - NCH + 2 else QUANT_LAG)
-            if not late:
-                for v in due("multiply", sent.get("quantise", 0) - 1):
-                    if v % 2 == 1:
-                        multiply([v - 1, v], False)
-            if not late:
-                for v in due("transpose", k - cast_lag + 1):
-                    p_transposes(v, 1)
-                    p_transposes(v, 0)
+            quant_lag = QUANT_LAG - 1 if k >= UNITS - NCH + 2 else QUANT_LAG
+            for v in due("multiply", sent.get("quantise", 0) - 1):
+                if v % 2 == 1:
+                    multiply([v - 1, v], False)
+            for v in due("transpose", k - CAST_LAG + 1):
+                p_transposes(v, 1)
+                p_transposes(v, 0)
             for v in due("normalise", k - 1):
                 recip(v)
                 normalise(v, "G" if v < UNITS - 2 else "V")
-            if k < UNITS:
-                exponent(k)
-            if not late:
-                for v in due("quantise", k - quant_lag):
-                    quantise(v)
+            exponent(k)
+            for v in due("quantise", k - quant_lag):
+                quantise(v)
             if u % NCH == 0:
                 fill(goal(k))
             elif k < 5:
@@ -544,14 +540,10 @@ def tile_neuralsort_t_kernel(tc, inp, scores, out_0, out_1, out_2):
             if live(u):
                 for h in range(2):
                     logits(u, h)
-            if late:
-                for v in due("transpose", k - 1):
-                    p_transposes(v, 1)
-                    p_transposes(v, 0)
-            for v in due("cast", k - cast_lag):
+            for v in due("cast", k - CAST_LAG):
                 cast(v, 1, "V" if v >= V_CASTS_FROM else "S")
                 cast(v, 0, "S")
-            if k % NCH == 1 and k < UNITS:
+            if k % NCH == 1:
                 quantise_input(k // NCH)
             if 2 <= k < 6:
                 regroup_input(k // 2 + 1, k % 2, "S")
@@ -559,16 +551,33 @@ def tile_neuralsort_t_kernel(tc, inp, scores, out_0, out_1, out_2):
             if u % NCH == NCH - 1 and u // NCH + 1 < B:
                 assert rb_ready[0] == u // NCH + 1
                 spread_rowsum(u // NCH + 1)
-            if late:
-                for v in due("quantise", k - quant_lag):
-                    quantise(v)
-                last = [[v] if v >= UNITS - 2 else [v - 1, v] for v in due("multiply", UNITS) if v >= UNITS - 2 or v % 2]
-                for units in last:
-                    multiply(units, True)
-                for n, units in enumerate(last):
-                    out_rows(units, "SV"[n % 2])
-            else:
-                for v in due("out", sent.get("multiply", 0) - 1):
-                    if v % 2 == 1:
-                        out_rows([v - 1, v], "V" if v >= V_OUT_FROM else "S")
+            for v in due("out", sent.get("multiply", 0) - 1):
+                if v % 2 == 1:
+                    out_rows([v - 1, v], "V" if v >= V_OUT_FROM else "S")
+
+        last = UNITS - 1
+        multiply([last - 5, last - 4], True)
+        p_transposes(last - 1, 0)
+        cast(last - 2, 1, "V")
+        cast(last - 2, 0, "S")
+        p_transposes(last - 1, 1)
+        recip(last)
+        quantise(last - 3)
+        normalise(last, "V")
+        out_rows([last - 5, last - 4], "S")
+        p_transposes(last, 0)
+        p_transposes(last, 1)
+        cast(last - 1, 0, "S")
+        cast(last - 1, 1, "V")
+        quantise(last - 2)
+        cast(last, 0, "S")
+        cast(last, 1, "V")
+        multiply([last - 3, last - 2], True)
+        quantise(last - 1)
+        multiply([last - 1], True)
+        out_rows([last - 3, last - 2], "S")
+        quantise(last)
+        multiply([last], True)
+        out_rows([last - 1], "S")
+        out_rows([last], "V")
         assert done[0] == len(queue)

@@ -20,7 +20,8 @@ HALF = 512
 UNITS = B * NCH
 FLOPS = 2 * B * DIM * DIM * Z
 AHEAD = 2
-V_CASTS_FROM = 20
+V_CASTS_FROM = 22
+V_CAST_SLOT = 5
 CAST_LAG = 3
 QUANT_LAG = 5
 V_OUT_FROM = 24
@@ -463,52 +464,43 @@ def tile_neuralsort_t_kernel(tc, inp, scores, out_0, out_1, out_2):
 
         groups = (
             (rowsum, (0, 1)), (rowsum, (2, 3)), (rowsum, (4,)),
-            (rank, (0, 1)), (rank, (2, 3, 4)), (rank, (5, 6)), (rank, (7, 8)), (rank, (9,)), (max_v, (0,)),
+            (rank, (0, 1)), (rank, (2, 3, 4)), (rank, (5, 6)), (rank, (7, 8)), (rank, (9,)),
         )
-        queue = []
 
-        def push_pieces(b, start, stop):
+        def group(b, n):
+            step_of, steps = groups[n]
+            for step in steps:
+                step_of(b, step)
+
+        def compare(b, start, stop):
             for n in range(start, stop):
-                queue.append(("cmp", b, n // 2, n % 2))
+                compare_v(b, n // 2, n % 2)
+                compare_pe(b, n // 2, n % 2)
 
-        push_pieces(1, 4, 2 * NCH)
-        for b in range(1, B):
-            if b + 1 < B:
-                push_pieces(b + 1, 0, 3)
-            for n in range(len(groups)):
-                queue.append(("group", b, n, 0))
-                if b + 1 < B and n + 3 < 2 * NCH:
-                    push_pieces(b + 1, n + 3, n + 4)
-            if b + 1 < B:
-                push_pieces(b + 1, len(groups) + 3, 2 * NCH)
-        done = [0]
-        rb_ready = [0]
+        def chain_before(k):
+            b, pos = k // NCH + 1, k % NCH
+            if b < B:
+                if pos >= 4:
+                    group(b, 2 * (pos - 4))
+                elif b == 1:
+                    compare(b, 3 * pos + 4, 3 * pos + 5)
 
-        def fill(goal):
-            while done[0] < min(goal, len(queue)):
-                kind, b, x, y = queue[done[0]]
-                done[0] += 1
-                if kind == "cmp":
-                    compare_v(b, x, y)
-                    compare_pe(b, x, y)
-                else:
-                    step_of, steps = groups[x]
-                    for step in steps:
-                        step_of(b, step)
-                    if step_of is rowsum and steps == (4,):
-                        rb_ready[0] = b
-                    if step_of is rank and steps == (9,):
+        def chain_behind(k):
+            b, pos = k // NCH + 1, k % NCH
+            if b < B:
+                if pos >= 4:
+                    group(b, 2 * (pos - 4) + 1)
+                    if pos == 5:
+                        spread_rowsum(b)
+                    if pos == 7:
                         max_pe(b)
+                elif b == 1:
+                    compare(b, 3 * pos + 5, 3 * pos + 7)
+                else:
+                    compare(b, 4 * pos, 4 * pos + 4)
 
         def live(u):
             return 0 <= u < UNITS
-
-        per_batch = 2 * NCH + len(groups)
-
-        def goal(k):
-            if k < 4:
-                return 4 * (k + 1)
-            return 3 * NCH + per_batch * (k - 4) // NCH
 
         sent = {}
 
@@ -531,26 +523,26 @@ def tile_neuralsort_t_kernel(tc, inp, scores, out_0, out_1, out_2):
                 recip(v)
                 normalise(v, "G" if v < UNITS - 2 else "V")
             exponent(k)
-            for v in due("quantise", k - quant_lag):
-                quantise(v)
-            if u % NCH == 0:
-                fill(goal(k))
-            elif k < 5:
-                fill(goal(k) - 1)
+            joint = k % NCH == NCH - 1 and k // NCH + 1 < B
+            if not joint:
+                for v in due("quantise", k - quant_lag):
+                    quantise(v)
+            chain_before(k)
             if live(u):
                 for h in range(2):
                     logits(u, h)
             for v in due("cast", k - CAST_LAG):
-                cast(v, 1, "V" if v >= V_CASTS_FROM else "S")
+                cast(v, 1, "V" if v >= V_CASTS_FROM or k % NCH == V_CAST_SLOT else "S")
                 cast(v, 0, "S")
             if k % NCH == 1:
                 quantise_input(k // NCH)
             if 2 <= k < 6:
                 regroup_input(k // 2 + 1, k % 2, "S")
-            fill(goal(k))
-            if u % NCH == NCH - 1 and u // NCH + 1 < B:
-                assert rb_ready[0] == u // NCH + 1
-                spread_rowsum(u // NCH + 1)
+            chain_behind(k)
+            if joint:
+                for v in due("quantise", k - quant_lag):
+                    quantise(v)
+                max_v(k // NCH + 1, 0)
             for v in due("out", sent.get("multiply", 0) - 1):
                 if v % 2 == 1:
                     out_rows([v - 1, v], "V" if v >= V_OUT_FROM else "S")
@@ -580,4 +572,3 @@ def tile_neuralsort_t_kernel(tc, inp, scores, out_0, out_1, out_2):
         multiply([last], True)
         out_rows([last - 1], "S")
         out_rows([last], "V")
-        assert done[0] == len(queue)

from contextlib import ExitStack

import concourse.mybir as mybir
from concourse.masks import make_identity

F32 = mybir.dt.float32
BF16 = mybir.dt.bfloat16
I32 = mybir.dt.int32
U32 = mybir.dt.uint32
U8 = mybir.dt.uint8
FP8X4 = mybir.dt.float8_e4m3fn_x4
ALU = mybir.AluOpType
ACT = mybir.ActivationFunctionType
AX = mybir.AxisListType

B, DIM, Z = 4, 1024, 256
P = 128
NCH = DIM // P
HALF = 512
UNITS = B * NCH
FLOPS = 2 * B * DIM * DIM * Z
AHEAD = 2
V_CASTS_FROM = 22
V_CAST_SLOT = 5
CAST_LAG = 3
QUANT_LAG = 5
V_OUT_FROM = 24


def tile_neuralsort_t_kernel(tc, inp, scores, out_0, out_1, out_2):
    nc = tc.nc
    raw_v = out_2.rearrange("b (p a) i -> b p a i", a=NCH)
    ph_v = out_1.rearrange("b (p a) i -> b p a i", a=NCH)
    out_v = out_0.rearrange("b (p a) z -> b p a z", a=NCH)
    in_v = inp.rearrange("b (s p) z -> b p s z", p=P)

    with ExitStack() as ctx:
        ctx.enter_context(tc.manual_schedule())
        const = ctx.enter_context(tc.tile_pool(name="const", bufs=1))
        tpool = ctx.enter_context(tc.tile_pool(name="tpool", bufs=2))
        rawp = ctx.enter_context(tc.tile_pool(name="rawp", bufs=5))
        php = ctx.enter_context(tc.tile_pool(name="php", bufs=3))
        exp_pool = ctx.enter_context(tc.tile_pool(name="exp_pool", bufs=3))
        gpool = ctx.enter_context(tc.tile_pool(name="gpool", bufs=6))
        outp = ctx.enter_context(tc.tile_pool(name="outp", bufs=2))
        bsmall = ctx.enter_context(tc.tile_pool(name="bsmall", bufs=2))
        usmall = ctx.enter_context(tc.tile_pool(name="usmall", bufs=6))
        ps_rb = ctx.enter_context(tc.psum_pool(name="ps_rb", bufs=1))
        ps_pt = ctx.enter_context(tc.psum_pool(name="ps_pt", bufs=4))
        ps_acc = ctx.enter_context(tc.psum_pool(name="ps_acc", bufs=1))
        ps_small = ctx.enter_context(tc.psum_pool(name="ps_small", bufs=1))

        xz = const.tile([P, P], BF16, name="xz", tag="xz")
        nc.sync.dma_start(out=xz[0:32, :], in_=scores.rearrange("b (c p) -> (b c) p", p=P))
        scores_b = [const.tile([P, DIM], BF16, name="scores_b%d" % b, tag="scores_b%d" % b) for b in range(B)]
        in_raw = [const.tile([P, NCH, Z], BF16, name="in_raw%d" % b, tag="in_raw%d" % b) for b in range(B)]
        nc.scalar.dma_start(out=scores_b[0][:], in_=scores[0].partition_broadcast(P))
        nc.sync.dma_start(out=in_raw[0][:], in_=in_v[0])
        nc.sync.dma_start(out=scores_b[1][:], in_=scores[1].partition_broadcast(P))
        for b in range(1, B):
            nc.sync.dma_start(out=in_raw[b][:], in_=in_v[b])
        for b in range(2, B):
            nc.sync.dma_start(out=scores_b[b][:], in_=scores[b].partition_broadcast(P))

        nc.vector.memset(xz[32:64, :], 0.0)
        nc.vector.memset(xz[64:128, :], 0.0)
        ident_bf = const.tile([P, P], BF16, name="ident_bf", tag="ident_bf")
        make_identity(nc, ident_bf[:])
        ident = const.tile([P, P], F32, name="ident", tag="ident")
        make_identity(nc, ident[:])
        s_col = const.tile([P, NCH], F32, name="s_col", tag="s_col")
        nc.gpsimd.iota(
            s_col[:], pattern=[[-2, NCH]], base=2 * DIM - 1, channel_multiplier=-2 * NCH,
            allow_small_or_imprecise_dtypes=True,
        )
        rev_hi = const.tile([P, P], BF16, name="rev_hi", tag="rev_hi")
        nc.gpsimd.iota(
            rev_hi[:], pattern=[[-1, P]], base=P - 1, channel_multiplier=0, allow_small_or_imprecise_dtypes=True
        )
        rev_lo = const.tile([P, NCH], F32, name="rev_lo", tag="rev_lo")
        nc.gpsimd.iota(
            rev_lo[:], pattern=[[-1, NCH]], base=NCH - 1, channel_multiplier=0, allow_small_or_imprecise_dtypes=True
        )
        margin = const.tile([P, P], F32, name="margin", tag="margin")
        nc.gpsimd.memset(margin[:], -(2.0 ** -126))
        nc.gpsimd.affine_select(
            out=margin[:], in_=margin[:], pattern=[[-1, P]], compare_op=ALU.is_gt, fill=0.0,
            base=0, channel_multiplier=1,
        )
        ones_bf = const.tile([P, P], BF16, name="ones_bf", tag="ones_bf")
        nc.vector.memset(ones_bf[:], 1.0)
        parts = const.tile([P, B * NCH, 4], BF16, name="parts", tag="parts")
        nc.vector.memset(parts[:, :, 0:1], 1.0)

        sc_t = ps_small.tile([P, P], BF16, name="sc_t", tag="small")
        nc.tensor.transpose(sc_t[:], xz[:], ident_bf[:])
        score_col = const.tile([P, B * NCH], F32, name="score_col", tag="score_col")
        nc.vector.tensor_copy(out=score_col[:], in_=sc_t[:, 0 : B * NCH])
        e_col = const.tile([P, B * NCH], F32, name="e_col", tag="e_col")
        nc.scalar.activation(out=e_col[:], in_=sc_t[:, 0 : B * NCH], func=ACT.Exp)
        e_hi = const.tile([P, B * NCH], BF16, name="e_hi", tag="e_hi")
        nc.scalar.activation(out=e_hi[:], in_=sc_t[:, 0 : B * NCH], func=ACT.Exp)

        igrp = const.tile([P, B * 2, Z, 4], BF16, name="igrp", tag="igrp", align_bytes=64)
        icodes = const.tile([P, B * 2 * Z], U32, name="icodes", tag="icodes", align_bytes=64)
        iscl = const.tile([P, B * 2 * Z], U8, name="iscl", tag="iscl", align_bytes=64)
        rest1 = const.tile([P, B * NCH], F32, name="rest1", tag="rest1")
        t_all = const.tile([P, B], F32, name="t_all", tag="t_all")
        e_b = [const.tile([P, DIM], F32, name="e_b%d" % b, tag="e_b%d" % b) for b in range(B)]

        rows = {}

        def split_e(step):
            if step == 0:
                nc.vector.tensor_tensor(out=rest1[:], in0=e_col[:], in1=e_hi[:], op=ALU.subtract)
            elif step == 1:
                nc.vector.tensor_tensor(out=parts[:, :, 2], in0=e_col[:], in1=e_hi[:], op=ALU.subtract)
            elif step == 2:
                nc.vector.tensor_copy(out=parts[:, :, 1], in_=e_hi[:])
            else:
                nc.vector.tensor_tensor(out=parts[:, :, 3], in0=rest1[:], in1=parts[:, :, 2], op=ALU.subtract)

        def total_pe():
            tot = ps_pt.tile([P, B * NCH * 4], F32, name="tot", tag="pt")
            nc.tensor.matmul(
                tot[:], lhsT=ones_bf[:], rhs=parts[:].rearrange("p c t -> p (c t)"), start=True, stop=True
            )
            rows["tot"] = tot

        def total_v():
            nc.vector.tensor_reduce(
                out=t_all[:],
                in_=rows["tot"][:].rearrange("p (b c t) -> p b c t", b=B, t=4)[:, :, :, 1:4],
                axis=AX.XY,
                op=ALU.add,
            )

        def spread_e(b):
            nc.scalar.activation(out=e_b[b][:], in_=scores_b[b][:], func=ACT.Exp)

        def regroup_input(b, g, engine):
            src = in_raw[b][:, 4 * g : 4 * g + 4, :].rearrange("p t (c i) -> p c t i", i=4)
            dst = igrp[:, 2 * b + g, :, :].rearrange("p (c i) t -> p c t i", i=4)
            if engine == "S":
                nc.scalar.copy(out=dst, in_=src)
            else:
                nc.vector.tensor_copy(out=dst, in_=src)

        def quantise_input(b):
            nc.vector.quantize_mx(
                out=icodes[:, 2 * Z * b : 2 * Z * (b + 1)].bitcast(FP8X4),
                scales=iscl[:, 2 * Z * b : 2 * Z * (b + 1)],
                in_=igrp[:, 2 * b : 2 * b + 2, :, :].rearrange("p g z t -> p (g z t)"),
            )

        def compare_v(b, ca, h):
            if ca == 0 and h == 0:
                rows[("cmp", b)] = tpool.tile([P, NCH, DIM], BF16, name="cmp", tag="cmp")
            cmp = rows[("cmp", b)]
            score = score_col[:, NCH * b + ca : NCH * b + ca + 1]
            lo, hi = HALF * h, HALF * (h + 1)
            d0, d1 = min(max(P * ca, lo), hi), min(max(P * (ca + 1), lo), hi)
            if d0 > lo:
                nc.vector.tensor_scalar(
                    out=cmp[:, ca, lo:d0], in0=scores_b[b][:, lo:d0], scalar1=score, scalar2=None, op0=ALU.is_ge
                )
            if d1 > d0:
                nc.vector.scalar_tensor_tensor(
                    out=cmp[:, ca, d0:d1], in0=scores_b[b][:, d0:d1], scalar=score, in1=margin[:],
                    op0=ALU.subtract, op1=ALU.is_gt,
                )
            if hi > d1:
                nc.vector.tensor_scalar(
                    out=cmp[:, ca, d1:hi], in0=scores_b[b][:, d1:hi], scalar1=score, scalar2=None, op0=ALU.is_gt
                )

        def compare_pe(b, ca, h):
            if ca == 0 and h == 0:
                if b == 0:
                    rows["sums"] = ps_small.tile([P, 2, 4 * NCH * NCH], F32, name="sums", tag="small")
                sums = rows["sums"][:, b % 2, :]
                rows[("ls", b)] = sums.rearrange("p (c k t) -> p c k t", c=NCH, t=4)
                rows[("mx", b)] = sums[:, 0 : 2 * NCH]
            ls = rows[("ls", b)]
            for cb in range(4 * h, 4 * h + 4):
                nc.tensor.matmul(
                    ls[:, cb, ca, :], lhsT=rows[("cmp", b)][:, ca, P * cb : P * (cb + 1)],
                    rhs=parts[:, NCH * b + ca, :], start=True, stop=True,
                )

        def small(key, b, shape, dtype=F32):
            if (key, b) not in rows:
                rows[(key, b)] = bsmall.tile(shape, dtype, name=key, tag=key)
            return rows[(key, b)]

        def rowsum(b, step, c0=0, c1=NCH):
            ls = rows[("ls", b)]
            e = e_col[:, NCH * b + c0 : NCH * b + c1]
            cnt, below = small("cnt", b, [P, NCH]), small("below", b, [P, NCH])
            x1, x2 = small("x1", b, [P, NCH]), small("x2", b, [P, NCH])
            if step == 0:
                nc.vector.tensor_reduce(out=cnt[:, c0:c1], in_=ls[:, c0:c1, :, 0], axis=AX.X, op=ALU.add)
            elif step == 1:
                nc.vector.tensor_reduce(out=below[:, c0:c1], in_=ls[:, c0:c1, :, 1:4], axis=AX.XY, op=ALU.add)
            elif step == 2:
                nc.vector.scalar_tensor_tensor(
                    out=x1[:, c0:c1], in0=cnt[:, c0:c1], scalar=2.0, in1=e, op0=ALU.mult, op1=ALU.mult
                )
            elif step == 3:
                nc.vector.tensor_scalar(
                    out=x2[:, c0:c1], in0=below[:, c0:c1], scalar1=-2.0, scalar2=t_all[:, b : b + 1],
                    op0=ALU.mult, op1=ALU.add,
                )
            else:
                nc.vector.tensor_tensor(
                    out=small("rsum", b, [P, NCH])[:, c0:c1], in0=x1[:, c0:c1], in1=x2[:, c0:c1], op=ALU.add
                )

        def spread_rowsum(b, halves=(0, 1)):
            for h in halves:
                rb = ps_rb.tile([P, HALF], F32, name="rb%d" % h, tag="rb%d" % h)
                for c in range(4):
                    col = 4 * h + c
                    nc.tensor.transpose(
                        rb[:, P * c : P * (c + 1)],
                        rows[("rsum", b)][:, col : col + 1].to_broadcast([P, P]),
                        ident[:],
                    )
                rows[("rb", b, h)] = rb

        def rank(b, step):
            if step == 0:
                nc.vector.tensor_copy(out=small("cnt_i", b, [P, NCH], I32)[:], in_=rows[("cnt", b)][:])
            elif step == 1:
                nc.vector.tensor_tensor(
                    out=small("nm", b, [P, NCH])[:], in0=rows[("x2", b)][:],
                    in1=e_col[:, NCH * b : NCH * (b + 1)], op=ALU.subtract,
                )
            elif step == 2:
                nc.vector.tensor_scalar(
                    out=small("hl_i", b, [P, 2, NCH], I32)[:, 0, :], in0=rows[("cnt_i", b)][:], scalar1=3,
                    scalar2=None, op0=ALU.arith_shift_right,
                )
            elif step == 3:
                nc.vector.tensor_scalar(
                    out=rows[("hl_i", b)][:, 1, :], in0=rows[("cnt_i", b)][:], scalar1=7,
                    scalar2=None, op0=ALU.bitwise_and,
                )
            elif step == 5:
                nc.vector.tensor_copy(out=small("hl", b, [P, 2, NCH])[:], in_=rows[("hl_i", b)][:])
            elif step == 4:
                nc.vector.tensor_copy(out=small("mp", b, [P, NCH, 2], BF16)[:, :, 0], in_=rows[("nm", b)][:])
            elif step == 7:
                nc.vector.tensor_tensor(
                    out=small("oh_lo", b, [P, NCH, NCH], BF16)[:],
                    in0=rev_lo[:].unsqueeze(1).to_broadcast([P, NCH, NCH]),
                    in1=rows[("hl", b)][:, 1, :].unsqueeze(2).to_broadcast([P, NCH, NCH]),
                    op=ALU.is_equal,
                )
            elif step == 6:
                nc.vector.tensor_tensor(
                    out=rows[("mp", b)][:, :, 1], in0=rows[("nm", b)][:], in1=rows[("mp", b)][:, :, 0],
                    op=ALU.subtract,
                )
            elif step == 8:
                oh = tpool.tile([P, NCH, P], BF16, name="oh", tag="oh")
                rows[("oh", b)] = oh
                for c in range(NCH):
                    nc.vector.tensor_scalar(
                        out=oh[:, c, :], in0=rev_hi[:], scalar1=rows[("hl", b)][:, 0, c : c + 1],
                        scalar2=None, op0=ALU.is_equal,
                    )
            else:
                nc.vector.tensor_tensor(
                    out=small("moh", b, [P, NCH, 2, NCH], BF16)[:],
                    in0=rows[("oh_lo", b)][:].unsqueeze(2).to_broadcast([P, NCH, 2, NCH]),
                    in1=rows[("mp", b)][:].unsqueeze(3).to_broadcast([P, NCH, 2, NCH]),
                    op=ALU.mult,
                )

        def max_pe(b):
            for c in range(NCH):
                nc.tensor.matmul(
                    rows[("mx", b)], lhsT=rows[("oh", b)][:, c, :],
                    rhs=rows[("moh", b)][:, c, :, :].rearrange("p t a -> p (t a)"),
                    start=(c == 0), stop=(c == NCH - 1),
                )

        def max_v(b, step):
            nc.vector.tensor_reduce(
                out=small("negm", b, [P, NCH])[:], in_=rows[("mx", b)].rearrange("p (t a) -> p a t", t=2),
                axis=AX.X, op=ALU.add,
            )

        def store_rows(view, tile_sb, u):
            b, a = divmod(u, NCH)
            if u in (0, 1, UNITS - 2, UNITS - 1):
                nc.sync.dma_start(out=view[b, :, a, :], in_=tile_sb[:, a % 2, :])
            elif a % 2 == 1:
                nc.sync.dma_start(out=view[b, :, a - 1 : a + 1, :], in_=tile_sb[:])

        def logits(u, h):
            b, a = divmod(u, NCH)
            if a % 2 == 0 and h == 0:
                rows[("raw", u // 2)] = rawp.tile([P, 2, DIM], F32, name="raw_sb", tag="raw_sb")
            raw_sb = rows[("raw", u // 2)]
            nc.vector.scalar_tensor_tensor(
                out=raw_sb[:, a % 2, HALF * h : HALF * (h + 1)],
                in0=e_b[b][:, HALF * h : HALF * (h + 1)],
                scalar=s_col[:, a : a + 1],
                in1=rows[("rb", b, h)][:],
                op0=ALU.mult, op1=ALU.subtract,
            )
            if h == 1:
                store_rows(raw_v, raw_sb, u)

        def exponent(u):
            b, a = divmod(u, NCH)
            ex = exp_pool.tile([P, DIM], F32, name="ex", tag="ex")
            ssum = usmall.tile([P, 1], F32, name="ssum", tag="ssum")
            nc.scalar.activation(
                out=ex[:], in_=rows[("raw", u // 2)][:, a % 2, :], func=ACT.Exp,
                bias=rows[("negm", b)][:, a : a + 1], scale=1.0, accum_out=ssum[:],
            )
            rows[("ex", u)] = ex
            rows[("ssum", u)] = ssum

        def recip(u):
            rinv = usmall.tile([P, 1], F32, name="rinv", tag="rinv")
            nc.vector.reciprocal(rinv[:], rows[("ssum", u)][:])
            rows[("rinv", u)] = rinv

        def normalise(u, engine):
            a = u % NCH
            if a % 2 == 0:
                rows[("ph", u // 2)] = php.tile([P, 2, DIM], F32, name="ph_sb", tag="ph_sb")
            ph_sb = rows[("ph", u // 2)]
            if engine == "G":
                nc.gpsimd.tensor_scalar(
                    out=ph_sb[:, a % 2, :], in0=rows[("ex", u)][:], scalar1=rows[("rinv", u)][:], scalar2=0.0,
                    op0=ALU.mult, op1=ALU.add,
                )
            else:
                for h in range(2):
                    cols = slice(HALF * h, HALF * (h + 1))
                    nc.vector.tensor_scalar(
                        out=ph_sb[:, a % 2, cols], in0=rows[("ex", u)][:, cols], scalar1=rows[("rinv", u)][:],
                        scalar2=None, op0=ALU.mult,
                    )
            store_rows(ph_v, ph_sb, u)

        def p_transposes(u, g):
            a = u % NCH
            ph_sb = rows[("ph", u // 2)]
            pt = ps_pt.tile([P, 4, P], F32, name="pt", tag="pt")
            for t in range(4):
                lo = HALF * g + P * t
                nc.tensor.transpose(pt[:, t, :], ph_sb[:, a % 2, lo : lo + P], ident[:])
            rows[("pt", u, g)] = pt

        def cast(u, g, engine):
            if ("grp", u) not in rows:
                rows[("grp", u)] = gpool.tile([P, 2, P, 4], BF16, name="grp", tag="grp", align_bytes=64)
            src = rows[("pt", u, g)][:].rearrange("p t j -> p j t")
            if engine == "V":
                nc.vector.tensor_copy(out=rows[("grp", u)][:, g, :, :], in_=src)
            else:
                nc.scalar.copy(out=rows[("grp", u)][:, g, :, :], in_=src)

        def quantise(u):
            codes = gpool.tile([P, 2 * P], U32, name="codes", tag="codes", align_bytes=64)
            scl = gpool.tile([P, 2 * P], U8, name="scl", tag="scl", align_bytes=64)
            nc.vector.quantize_mx(
                out=codes[:].bitcast(FP8X4), scales=scl[:],
                in_=rows[("grp", u)][:].rearrange("p g j t -> p (g j t)"),
            )
            rows[("codes", u)] = (codes, scl)

        def multiply(units, late):
            if late:
                acc = ps_pt.tile([P, 2, Z], F32, name="acc_late", tag="pt")
            else:
                acc = ps_acc.tile([P, 2, Z], F32, name="acc", tag="acc")
            for w, u in enumerate(units):
                b = u // NCH
                codes, scl = rows[("codes", u)]
                for g in range(2):
                    lo = Z * (2 * b + g)
                    nc.tensor.matmul_mx(
                        out=acc[:, w, :],
                        lhsT=codes[:, P * g : P * (g + 1)].bitcast(FP8X4),
                        lhsT_scale=scl[:, P * g : P * (g + 1)],
                        rhs=icodes[:, lo : lo + Z].bitcast(FP8X4),
                        rhs_scale=iscl[:, lo : lo + Z],
                        start=(g == 0), stop=(g == 1),
                    )
            rows[("acc", units[-1])] = acc

        def out_rows(units, engine):
            b, a = divmod(units[0], NCH)
            n = len(units)
            if ("out", b) not in rows:
                rows[("out", b)] = outp.tile([P, NCH, Z], F32, name="out_sb", tag="out_sb")
            out_sb = rows[("out", b)]
            src = rows[("acc", units[-1])][:, 0:n, :]
            if engine == "V":
                nc.vector.tensor_copy(out=out_sb[:, a : a + n, :], in_=src)
            else:
                nc.scalar.copy(out=out_sb[:, a : a + n, :], in_=src)
            last = a + n
            if b == B - 1 and last > 4:
                nc.sync.dma_start(out=out_v[b, :, a:last, :], in_=out_sb[:, a:last, :])
            elif last % 4 == 0:
                nc.sync.dma_start(out=out_v[b, :, last - 4 : last, :], in_=out_sb[:, last - 4 : last, :])

        for h in range(2):
            for ca in range(NCH):
                compare_v(0, ca, h)
                if h == 0 and ca == 2:
                    for step in range(4):
                        split_e(step)
                    total_pe()
                    for c in range(3):
                        compare_pe(0, c, h)
                elif h == 1 or ca > 2:
                    compare_pe(0, ca, h)
        total_v()
        spread_e(0)
        for g in range(2):
            regroup_input(0, g, "S")
        spread_e(1)
        for g in range(2):
            regroup_input(1, g, "S")
        spread_e(2)
        spread_e(3)
        for steps in ((0, 1), (2, 3), (4,)):
            for h in range(2):
                for step in steps:
                    rowsum(0, step, 4 * h, 4 * h + 4)
                if steps == (4,):
                    spread_rowsum(0, (h,))
        rank(0, 0)
        rank(0, 1)
        compare_v(1, 0, 0)
        for step in (2, 3, 4):
            rank(0, step)
        logits(0, 0)
        rank(0, 5)
        rank(0, 6)
        logits(0, 1)
        rank(0, 7)
        rank(0, 8)
        compare_v(1, 0, 1)
        rank(0, 9)
        max_pe(0)
        compare_v(1, 1, 0)
        compare_v(1, 1, 1)
        max_v(0, 0)
        for n in range(4):
            compare_pe(1, n // 2, n % 2)
        for u in range(1, AHEAD):
            for h in range(2):
                logits(u, h)

        groups = (
            (rowsum, (0, 1)), (rowsum, (2, 3)), (rowsum, (4,)),
            (rank, (0, 1)), (rank, (2, 3, 4)), (rank, (5, 6)), (rank, (7, 8)), (rank, (9,)),
        )

        def group(b, n):
            step_of, steps = groups[n]
            for step in steps:
                step_of(b, step)

        def compare(b, start, stop):
            for n in range(start, stop):
                compare_v(b, n // 2, n % 2)
                compare_pe(b, n // 2, n % 2)

        def chain_before(k):
            b, pos = k // NCH + 1, k % NCH
            if b < B:
                if pos >= 4:
                    group(b, 2 * (pos - 4))
                elif b == 1:
                    compare(b, 3 * pos + 4, 3 * pos + 5)

        def chain_behind(k):
            b, pos = k // NCH + 1, k % NCH
            if b < B:
                if pos >= 4:
                    group(b, 2 * (pos - 4) + 1)
                    if pos == 5:
                        spread_rowsum(b)
                    if pos == 7:
                        max_pe(b)
                elif b == 1:
                    compare(b, 3 * pos + 5, 3 * pos + 7)
                else:
                    compare(b, 4 * pos, 4 * pos + 4)

        def live(u):
            return 0 <= u < UNITS

        sent = {}

        def due(stage, limit):
            first = sent.get(stage, 0)
            last = min(limit, UNITS - 1)
            sent[stage] = max(first, last + 1)
            return range(first, last + 1)

        for k in range(UNITS):
            u = k + AHEAD
            quant_lag = QUANT_LAG - 1 if k >= UNITS - NCH + 2 else QUANT_LAG
            for v in due("multiply", sent.get("quantise", 0) - 1):
                if v % 2 == 1:
                    multiply([v - 1, v], False)
            for v in due("transpose", k - CAST_LAG + 1):
                p_transposes(v, 1)
                p_transposes(v, 0)
            for v in due("normalise", k - 1):
                recip(v)
                normalise(v, "G" if v < UNITS - 2 else "V")
            exponent(k)
            joint = k % NCH == NCH - 1 and k // NCH + 1 < B
            if not joint:
                for v in due("quantise", k - quant_lag):
                    quantise(v)
            chain_before(k)
            if live(u):
                for h in range(2):
                    logits(u, h)
            for v in due("cast", k - CAST_LAG):
                cast(v, 1, "V" if v >= V_CASTS_FROM or k % NCH == V_CAST_SLOT else "S")
                cast(v, 0, "S")
            if k % NCH == 1:
                quantise_input(k // NCH)
            if 2 <= k < 6:
                regroup_input(k // 2 + 1, k % 2, "S")
            chain_behind(k)
            if joint:
                for v in due("quantise", k - quant_lag):
                    quantise(v)
                max_v(k // NCH + 1, 0)
            for v in due("out", sent.get("multiply", 0) - 1):
                if v % 2 == 1:
                    out_rows([v - 1, v], "V" if v >= V_OUT_FROM else "S")

        last = UNITS - 1
        multiply([last - 5, last - 4], True)
        p_transposes(last - 1, 0)
        cast(last - 2, 1, "V")
        cast(last - 2, 0, "S")
        p_transposes(last - 1, 1)
        recip(last)
        quantise(last - 3)
        normalise(last, "V")
        out_rows([last - 5, last - 4], "S")
        p_transposes(last, 0)
        p_transposes(last, 1)
        cast(last - 1, 0, "S")
        cast(last - 1, 1, "V")
        quantise(last - 2)
        cast(last, 0, "S")
        cast(last, 1, "V")
        multiply([last - 3, last - 2], True)
        quantise(last - 1)
        multiply([last - 1], True)
        out_rows([last - 3, last - 2], "S")
        quantise(last)
        multiply([last], True)
        out_rows([last - 1], "S")
        out_rows([last], "V")
